import numpy as np
import ml_dtypes


def mxq(x, axis, fmt="e4m3"):
    dtype, down = {"e4m3": (ml_dtypes.float8_e4m3fn, 7), "e5m2": (ml_dtypes.float8_e5m2, 14)}[fmt]
    v = np.moveaxis(np.asarray(x, np.float32).astype(ml_dtypes.bfloat16).astype(np.float64), axis, -1)
    blocks = v.reshape(v.shape[:-1] + (-1, 32))
    amax = np.abs(blocks).max(-1, keepdims=True)
    byte = np.maximum(np.where(amax > 0, np.frexp(amax)[1] - 1 + 127, 0) - down, 1)
    scale = np.exp2(byte - 127.0)
    codes = (blocks / scale).astype(np.float32).astype(dtype).astype(np.float64)
    return np.moveaxis((codes * scale).reshape(v.shape), -1, axis)


WIDE = False


def mx_kscale(k):
    if not WIDE:
        return np.ones(k)
    levels = np.array([10, -10, 5, -5, 0])
    a = np.random.permutation(np.resize(levels, k // 512 * 4)).reshape(k // 512, 4)
    idx = np.arange(k)
    return np.exp2(a[idx // 512, idx % 128 // 32])


BF16 = ml_dtypes.bfloat16


def bf(x):
    return np.asarray(x, np.float32).astype(BF16)


def f64(x):
    return np.asarray(x).astype(np.float64)


E2M1 = np.array([0.0, 0.5, 1.0, 1.5, 2.0, 3.0, 4.0, 6.0, -0.0, -0.5, -1.0, -1.5, -2.0, -3.0, -4.0, -6.0])


def pack_weight(w, fmt):
    k, n = w.shape
    w = f64(bf(w)).reshape(k // 32, 32, n)
    amax = np.abs(w).max(1)
    if fmt == "e4m3":
        byte = np.frexp(amax)[1] - 1 + 127 - 7
    else:
        mant, ex = np.frexp(amax / 6.0)
        byte = np.where(mant > 0.5, ex, ex - 1) + 127
    byte = np.clip(np.where(amax > 0, byte, 1), 1, 254)
    scaled = (w * np.exp2(127.0 - byte)[:, None, :]).reshape(k, n).astype(np.float32)
    by_word = np.ascontiguousarray(scaled.reshape(k // 512, 128, 4, n).transpose(0, 1, 3, 2))
    if fmt == "e4m3":
        words = by_word.astype(ml_dtypes.float8_e4m3fn).view(np.uint8)
    else:
        c = by_word.astype(ml_dtypes.float4_e2m1fn).view(np.uint8) & 0xF
        words = c[..., 0::2] | (c[..., 1::2] << 4)
    return np.ascontiguousarray(words), np.ascontiguousarray(byte.astype(np.uint8).reshape(k // 512, 16, n))


def unpack_weight(words, scales, fmt):
    g, p, n, _ = words.shape
    if fmt == "e4m3":
        vals = np.ascontiguousarray(words).view(ml_dtypes.float8_e4m3fn).astype(np.float64)
    else:
        nib = np.empty((g, p, n, 4), np.uint8)
        nib[..., 0::2] = words & 0xF
        nib[..., 1::2] = words >> 4
        vals = E2M1[nib]
    vals = vals * np.repeat(np.exp2(scales.astype(np.float64) - 127.0), 8, axis=1)[..., None]
    return vals.transpose(0, 1, 3, 2).reshape(g * 512, n)


B, IN, H = 2048, 512, 512
G = 4 * H
EPS = 1e-5
FMT = "e4m3"


def _layernorm(v, gamma, beta):
    mean = np.mean(v, axis=-1, keepdims=True)
    var = np.mean(np.square(v - mean), axis=-1, keepdims=True)
    return (v - mean) / np.sqrt(var + EPS) * gamma + beta


def sigmoid(v):
    return 1.0 / (1.0 + np.exp(-v))


def setup_inputs():
    s, t = mx_kscale(IN), mx_kscale(H)
    x = bf(np.random.standard_normal((B, IN)) * s)
    h_prev = bf(np.random.standard_normal((B, H)) * t)
    c_prev = bf(np.random.standard_normal((B, H)))
    W_ih_words, W_ih_scales = pack_weight(np.random.standard_normal((IN, G)) / np.sqrt(IN) / s[:, None], FMT)
    W_hh_words, W_hh_scales = pack_weight(np.random.standard_normal((H, G)) / np.sqrt(H) / t[:, None], FMT)
    return {
        "x": x,
        "h_prev": h_prev,
        "c_prev": c_prev,
        "W_ih_words": W_ih_words,
        "W_ih_scales": W_ih_scales,
        "W_hh_words": W_hh_words,
        "W_hh_scales": W_hh_scales,
        "gamma_ih": bf(1.0 + 0.2 * np.random.standard_normal(G)),
        "beta_ih": bf(0.3 * np.random.standard_normal(G)),
        "gamma_hh": bf(1.0 + 0.2 * np.random.standard_normal(G)),
        "beta_hh": bf(0.3 * np.random.standard_normal(G)),
        "gamma_c": bf(1.0 + 0.2 * np.random.standard_normal(H)),
        "beta_c": bf(0.3 * np.random.standard_normal(H)),
    }


def reference(x, h_prev, c_prev, W_ih_words, W_ih_scales, W_hh_words, W_hh_scales, gamma_ih, beta_ih, gamma_hh, beta_hh, gamma_c, beta_c):
    a_ih = mxq(f64(x), 1, "e4m3") @ unpack_weight(W_ih_words, W_ih_scales, FMT)
    a_hh = mxq(f64(h_prev), 1, "e4m3") @ unpack_weight(W_hh_words, W_hh_scales, FMT)
    gates_ih = _layernorm(a_ih, f64(gamma_ih), f64(beta_ih))
    gates_hh = _layernorm(a_hh, f64(gamma_hh), f64(beta_hh))
    gates = gates_ih + gates_hh
    i_g, f_g, g_g, o_g = np.split(gates, 4, axis=1)
    i_t = sigmoid(i_g)
    f_t = sigmoid(f_g)
    g_t = np.tanh(g_g)
    o_t = sigmoid(o_g)
    c_t = f_t * f64(c_prev) + i_t * g_t
    h_t = o_t * np.tanh(_layernorm(c_t, f64(gamma_c), f64(beta_c)))
    return (h_t, c_t)

@@ -1,0 +1,345 @@
+from contextlib import ExitStack
+
+import concourse.mybir as mybir
+from concourse.masks import make_identity
+
+F32 = mybir.dt.float32
+BF16 = mybir.dt.bfloat16
+I32 = mybir.dt.int32
+U32 = mybir.dt.uint32
+U8 = mybir.dt.uint8
+FP8X4 = mybir.dt.float8_e4m3fn_x4
+ALU = mybir.AluOpType
+ACT = mybir.ActivationFunctionType
+AX = mybir.AxisListType
+
+P = 128
+B = 2048
+K = 512
+H = 512
+G = 4 * H
+EPS = 1e-5
+ROW_TILES = B // P
+BANK = 512
+BANKS = G // BANK
+FOLD = 128
+LOAD_TILES = 4
+
+FLOPS = 2 * 2 * B * K * G
+
+
+def tile_layernormlstmcell_kernel(
+    tc,
+    x,
+    h_prev,
+    c_prev,
+    W_ih_words,
+    W_ih_scales,
+    W_hh_words,
+    W_hh_scales,
+    gamma_ih,
+    beta_ih,
+    gamma_hh,
+    beta_hh,
+    gamma_c,
+    beta_c,
+    out_0,
+    out_1,
+):
+    nc = tc.nc
+    with ExitStack() as ctx:
+        const = ctx.enter_context(tc.tile_pool(name="const", bufs=1))
+        stage = ctx.enter_context(tc.tile_pool(name="stage", bufs=2))
+        operand = ctx.enter_context(tc.tile_pool(name="operand", bufs=4))
+        stats = ctx.enter_context(tc.tile_pool(name="stats", bufs=4))
+        wide = ctx.enter_context(tc.tile_pool(name="wide", bufs=3))
+        narrow = ctx.enter_context(tc.tile_pool(name="narrow", bufs=3))
+        psum_flip = ctx.enter_context(tc.psum_pool(name="psum_flip", bufs=1))
+        psum_fold = ctx.enter_context(tc.psum_pool(name="psum_fold", bufs=1))
+        psum_acc = ctx.enter_context(tc.psum_pool(name="psum_acc", bufs=6))
+
+        x_rows = x.rearrange("(p t) k -> p t k", t=ROW_TILES)
+        h_rows = h_prev.rearrange("(p t) k -> p t k", t=ROW_TILES)
+        c_rows = c_prev.rearrange("(p t) k -> p t k", t=ROW_TILES)
+        h_out = out_0.rearrange("(p t) k -> p t k", t=ROW_TILES)
+        c_out = out_1.rearrange("(p t) k -> p t k", t=ROW_TILES)
+
+        zero = const.tile([P, 1], F32)
+        nc.vector.memset(zero[:], 0.0)
+        warm = const.tile([P, 1], F32)
+        nc.scalar.activation(out=warm[:], in_=zero[:], func=ACT.Sigmoid)
+
+        minus_half = const.tile([P, 2], F32)
+        nc.vector.memset(minus_half[:], -0.5)
+        ident = const.tile([P, P], F32)
+        make_identity(nc, ident[:])
+
+        w_scales = [
+            const.tile([P, G], U8, name="w_ih_scales", align_bytes=64),
+            const.tile([P, G], U8, name="w_hh_scales", align_bytes=64),
+        ]
+        for plane in w_scales:
+            nc.vector.memset(plane[:].bitcast(I32), 0)
+
+        x_sb = const.tile([P, ROW_TILES, K], BF16)
+        h_sb = const.tile([P, ROW_TILES, K], BF16)
+        c_sb = const.tile([P, ROW_TILES, H], BF16)
+        first = slice(0, LOAD_TILES)
+        nc.sync.dma_start(out=x_sb[:, first, :], in_=x_rows[:, first, :])
+        nc.sync.dma_start(out=h_sb[:, first, :], in_=h_rows[:, first, :])
+
+        for plane, rows in zip(w_scales, (W_ih_scales[0], W_hh_scales[0])):
+            for quad in range(4):
+                nc.sync.dma_start(
+                    out=plane[32 * quad : 32 * quad + 4, :].bitcast(I32),
+                    in_=rows[4 * quad : 4 * quad + 4, :].bitcast(I32),
+                )
+
+        w_words = [
+            const.tile([P, 4 * G], U8, name="w_ih_words", align_bytes=64),
+            const.tile([P, 4 * G], U8, name="w_hh_words", align_bytes=64),
+        ]
+        for words, source in zip(w_words, (W_ih_words[0], W_hh_words[0])):
+            nc.sync.dma_start(
+                out=words[:].bitcast(I32),
+                in_=source.rearrange("p n t -> p (n t)").bitcast(I32),
+            )
+        nc.sync.dma_start(out=c_sb[:, first, :], in_=c_rows[:, first, :])
+        for start in range(LOAD_TILES, ROW_TILES, LOAD_TILES):
+            chunk = slice(start, start + LOAD_TILES)
+            nc.sync.dma_start(out=x_sb[:, chunk, :], in_=x_rows[:, chunk, :])
+            nc.sync.dma_start(out=h_sb[:, chunk, :], in_=h_rows[:, chunk, :])
+            nc.sync.dma_start(out=c_sb[:, chunk, :], in_=c_rows[:, chunk, :])
+
+        gamma = [
+            const.tile([P, G], BF16, name="gamma_ih_sb"),
+            const.tile([P, G], BF16, name="gamma_hh_sb"),
+        ]
+        nc.scalar.dma_start(out=gamma[0][:], in_=gamma_ih.partition_broadcast(P))
+        nc.scalar.dma_start(out=gamma[1][:], in_=gamma_hh.partition_broadcast(P))
+        beta_ih_sb = const.tile([P, G], BF16)
+        beta_hh_sb = const.tile([P, G], BF16)
+        nc.scalar.dma_start(out=beta_ih_sb[:], in_=beta_ih.partition_broadcast(P))
+        nc.scalar.dma_start(out=beta_hh_sb[:], in_=beta_hh.partition_broadcast(P))
+        gamma_c_sb = const.tile([P, H], BF16)
+        beta_c_sb = const.tile([P, H], BF16)
+        nc.scalar.dma_start(out=gamma_c_sb[:], in_=gamma_c.partition_broadcast(P))
+        nc.scalar.dma_start(out=beta_c_sb[:], in_=beta_c.partition_broadcast(P))
+        beta_sum = const.tile([P, G], F32)
+        nc.gpsimd.tensor_tensor(
+            out=beta_sum[:], in0=beta_ih_sb[:], in1=beta_hh_sb[:], op=ALU.add
+        )
+
+        grouped = {}
+        rows_mx = {}
+        neg_mean = {}
+        sq_part = {}
+        scaled = {}
+        rstd = {}
+        o_gate = {}
+        c_new = {}
+        neg_mean_c = {}
+        rstd_c = {}
+        normed = {}
+
+        def flip_rows(t):
+            flipped = psum_flip.tile([P, 2, 2, P], F32)
+            for s, rows in enumerate((x_sb, h_sb)):
+                words = rows[:, t, :].bitcast(F32)
+                for u in range(2):
+                    nc.tensor.transpose(flipped[:, s, u, :], words[:, u : K // 2 : 2], ident[:])
+            grouped[t] = stage.tile([P, 2, P, 4], BF16, name="grouped", align_bytes=64)
+            nc.scalar.copy(
+                out=grouped[t][:].bitcast(F32), in_=flipped[:].rearrange("p s u r -> p s r u")
+            )
+
+        def quantise_rows(t):
+            codes = operand.tile([P, 2 * P], U32, align_bytes=64)
+            scales = operand.tile([P, 2 * P], U8, align_bytes=64)
+            nc.vector.quantize_mx(
+                out=codes[:].bitcast(FP8X4),
+                scales=scales[:],
+                in_=grouped[t][:].rearrange("p s r t -> p (s r t)"),
+            )
+            rows_mx[t] = (codes, scales)
+
+        def mx_pass(out, t, s, col, width, start, stop):
+            codes, scales = rows_mx[t]
+            rows = slice(s * P, (s + 1) * P)
+            nc.tensor.matmul_mx(
+                out=out,
+                lhsT=codes[:, rows].bitcast(FP8X4),
+                lhsT_scale=scales[:, rows],
+                rhs=w_words[s][:, 4 * col : 4 * (col + width)].bitcast(FP8X4),
+                rhs_scale=w_scales[s][:, col : col + width],
+                start=start,
+                stop=stop,
+            )
+
+        def inverse_std(sq_sum, count, width):
+            var = stats.tile([P, width], F32, name="var", tag="var%d" % width)
+            nc.vector.tensor_scalar(
+                out=var[:], in0=sq_sum, scalar1=1.0 / count, scalar2=EPS, op0=ALU.mult, op1=ALU.add
+            )
+            result = stats.tile([P, width], F32, name="rstd", tag="rstd%d" % width)
+            nc.gpsimd.tensor_tensor(
+                out=result[:], in0=var[:], in1=minus_half[:, 0:width], op=ALU.pow
+            )
+            return result
+
+        def row_means(t):
+            fold = psum_fold.tile([P, 2, FOLD], F32)
+            for s in range(2):
+                for j in range(G // FOLD):
+                    mx_pass(fold[:, s, :], t, s, j * FOLD, FOLD, j == 0, j == G // FOLD - 1)
+            neg_mean[t] = stats.tile([P, 2], F32, name="neg_mean")
+            for s in range(2):
+                scrap = stage.tile([P, BANK], BF16, name="scrap")
+                nc.scalar.activation(
+                    out=scrap[:, 0:FOLD],
+                    in_=fold[:, s, :],
+                    func=ACT.Copy,
+                    scale=-1.0 / G,
+                    accum_out=neg_mean[t][:, s : s + 1],
+                )
+
+        def products(t):
+            sq_part[t] = stats.tile([P, 2, BANKS], F32, name="sq_part")
+            scaled[t] = (
+                wide.tile([P, G], F32, name="scaled_ih"),
+                wide.tile([P, G], F32, name="scaled_hh"),
+            )
+            for s in range(2):
+                for j in range(BANKS):
+                    cols = slice(j * BANK, (j + 1) * BANK)
+                    acc = psum_acc.tile([P, BANK], F32)
+                    mx_pass(acc[:], t, s, j * BANK, BANK, True, True)
+                    nc.vector.scalar_tensor_tensor(
+                        out=scaled[t][s][:, cols],
+                        in0=acc[:],
+                        scalar=neg_mean[t][:, s : s + 1],
+                        in1=gamma[s][:, cols],
+                        op0=ALU.add,
+                        op1=ALU.mult,
+                    )
+                    scrap = stage.tile([P, BANK], BF16, name="scrap")
+                    nc.scalar.activation(
+                        out=scrap[:],
+                        in_=acc[:],
+                        func=ACT.Square,
+                        bias=neg_mean[t][:, s : s + 1],
+                        accum_out=sq_part[t][:, s, j : j + 1],
+                    )
+
+        def gate_rstd(t):
+            sq_sum = stats.tile([P, 2], F32)
+            nc.vector.tensor_reduce(out=sq_sum[:], in_=sq_part[t][:], axis=AX.X, op=ALU.add)
+            rstd[t] = inverse_std(sq_sum[:], G, 2)
+
+        def combine(t):
+            scaled_ih, scaled_hh = scaled[t]
+            nc.vector.scalar_tensor_tensor(
+                out=scaled_hh[:],
+                in0=scaled_hh[:],
+                scalar=rstd[t][:, 1:2],
+                in1=beta_sum[:],
+                op0=ALU.mult,
+                op1=ALU.add,
+            )
+            nc.vector.scalar_tensor_tensor(
+                out=scaled_ih[:],
+                in0=scaled_ih[:],
+                scalar=rstd[t][:, 0:1],
+                in1=scaled_hh[:],
+                op0=ALU.mult,
+                op1=ALU.add,
+            )
+
+        def gate_functions(t):
+            gates = scaled[t][0]
+            nc.scalar.activation(out=gates[:, 0 : 2 * H], in_=gates[:, 0 : 2 * H], func=ACT.Sigmoid)
+            nc.scalar.activation(
+                out=gates[:, 2 * H : 3 * H], in_=gates[:, 2 * H : 3 * H], func=ACT.Tanh
+            )
+            o_gate[t] = narrow.tile([P, H], F32, name="o_gate")
+            nc.scalar.activation(out=o_gate[t][:], in_=gates[:, 3 * H : 4 * H], func=ACT.Sigmoid)
+
+        def cell_state(t):
+            gates = scaled[t][0]
+            kept = narrow.tile([P, H], F32)
+            nc.gpsimd.tensor_tensor(
+                out=kept[:], in0=gates[:, H : 2 * H], in1=c_sb[:, t, :], op=ALU.mult
+            )
+            c_new[t] = narrow.tile([P, H], F32, name="c_new")
+            nc.gpsimd.tensor_tensor(
+                out=c_new[t][:], in0=gates[:, 0:H], in1=gates[:, 2 * H : 3 * H], op=ALU.mult
+            )
+            nc.gpsimd.tensor_tensor(out=c_new[t][:], in0=c_new[t][:], in1=kept[:], op=ALU.add)
+            nc.sync.dma_start(out=c_out[:, t, :], in_=c_new[t][:])
+
+        def cell_stats(t):
+            neg_mean_c[t] = stats.tile([P, 1], F32, name="neg_mean_c")
+            scrap = stage.tile([P, BANK], BF16, name="scrap")
+            nc.scalar.activation(
+                out=scrap[:],
+                in_=c_new[t][:],
+                func=ACT.Copy,
+                scale=-1.0 / H,
+                accum_out=neg_mean_c[t][:],
+            )
+            sq_sum = stats.tile([P, 1], F32, name="sq_sum_c")
+            scrap = stage.tile([P, BANK], BF16, name="scrap")
+            nc.scalar.activation(
+                out=scrap[:],
+                in_=c_new[t][:],
+                func=ACT.Square,
+                bias=neg_mean_c[t][:],
+                accum_out=sq_sum[:],
+            )
+            rstd_c[t] = inverse_std(sq_sum[:], H, 1)
+
+        def cell_norm(t):
+            normed[t] = narrow.tile([P, H], F32, name="normed")
+            nc.vector.scalar_tensor_tensor(
+                out=normed[t][:],
+                in0=c_new[t][:],
+                scalar=neg_mean_c[t][:],
+                in1=gamma_c_sb[:],
+                op0=ALU.add,
+                op1=ALU.mult,
+            )
+            nc.vector.scalar_tensor_tensor(
+                out=normed[t][:],
+                in0=normed[t][:],
+                scalar=rstd_c[t][:],
+                in1=beta_c_sb[:],
+                op0=ALU.mult,
+                op1=ALU.add,
+            )
+
+        def cell_tanh(t):
+            nc.scalar.activation(out=normed[t][:], in_=normed[t][:], func=ACT.Tanh)
+
+        def hidden_out(t):
+            h_new = narrow.tile([P, H], F32)
+            nc.gpsimd.tensor_tensor(out=h_new[:], in0=o_gate[t][:], in1=normed[t][:], op=ALU.mult)
+            nc.sync.dma_start(out=h_out[:, t, :], in_=h_new[:])
+
+        def on(stage_of, t):
+            if 0 <= t < ROW_TILES:
+                stage_of(t)
+
+        with tc.manual_schedule():
+            for i in range(-2, ROW_TILES + 3):
+                on(gate_rstd, i - 1)
+                on(cell_norm, i - 3)
+                on(gate_functions, i - 2)
+                on(cell_tanh, i - 3)
+                on(flip_rows, i + 2)
+                on(row_means, i + 1)
+                on(products, i)
+                on(quantise_rows, i + 2)
+                on(combine, i - 1)
+                on(cell_state, i - 2)
+                on(hidden_out, i - 3)
+                on(cell_stats, i - 2)

@@ -69,7 +69,7 @@ def tile_layernormlstmcell_kernel(
         warm = const.tile([P, 1], F32)
         nc.scalar.activation(out=warm[:], in_=zero[:], func=ACT.Sigmoid)
 
-        minus_half = const.tile([P, 2], F32)
+        minus_half = const.tile([P, 3], F32)
         nc.vector.memset(minus_half[:], -0.5)
         ident = const.tile([P, P], F32)
         make_identity(nc, ident[:])
@@ -139,6 +139,7 @@ def tile_layernormlstmcell_kernel(
         o_gate = {}
         c_new = {}
         neg_mean_c = {}
+        sq_sum_c = {}
         rstd_c = {}
         normed = {}
 
@@ -175,17 +176,6 @@ def tile_layernormlstmcell_kernel(
                 start=start,
                 stop=stop,
             )
-
-        def inverse_std(sq_sum, count, width):
-            var = stats.tile([P, width], F32, name="var", tag="var%d" % width)
-            nc.vector.tensor_scalar(
-                out=var[:], in0=sq_sum, scalar1=1.0 / count, scalar2=EPS, op0=ALU.mult, op1=ALU.add
-            )
-            result = stats.tile([P, width], F32, name="rstd", tag="rstd%d" % width)
-            nc.gpsimd.tensor_tensor(
-                out=result[:], in0=var[:], in1=minus_half[:, 0:width], op=ALU.pow
-            )
-            return result
 
         def row_means(t):
             fold = psum_fold.tile([P, 2, FOLD], F32)
@@ -231,29 +221,62 @@ def tile_layernormlstmcell_kernel(
                         accum_out=sq_part[t][:, s, j : j + 1],
                     )
 
-        def gate_rstd(t):
-            sq_sum = stats.tile([P, 2], F32)
-            nc.vector.tensor_reduce(out=sq_sum[:], in_=sq_part[t][:], axis=AX.X, op=ALU.add)
-            rstd[t] = inverse_std(sq_sum[:], G, 2)
+        def inverse_stds(gate_tile, cell_tile):
+            gates_live = 0 <= gate_tile < ROW_TILES
+            cell_live = 0 <= cell_tile < ROW_TILES
+            if not (gates_live or cell_live):
+                return
+            var = stats.tile([P, 3], F32)
+            if gates_live:
+                sq_sum = stats.tile([P, 2], F32)
+                nc.vector.tensor_reduce(
+                    out=sq_sum[:], in_=sq_part[gate_tile][:], axis=AX.X, op=ALU.add
+                )
+                nc.vector.tensor_scalar(
+                    out=var[:, 0:2],
+                    in0=sq_sum[:],
+                    scalar1=1.0 / G,
+                    scalar2=EPS,
+                    op0=ALU.mult,
+                    op1=ALU.add,
+                )
+            if cell_live:
+                nc.vector.tensor_scalar(
+                    out=var[:, 2:3],
+                    in0=sq_sum_c[cell_tile][:],
+                    scalar1=1.0 / H,
+                    scalar2=EPS,
+                    op0=ALU.mult,
+                    op1=ALU.add,
+                )
+            live = slice(0 if gates_live else 2, 3 if cell_live else 2)
+            result = stats.tile([P, 3], F32)
+            nc.gpsimd.tensor_tensor(
+                out=result[:, live], in0=var[:, live], in1=minus_half[:, live], op=ALU.pow
+            )
+            rstd[gate_tile] = result[:, 0:2]
+            rstd_c[cell_tile] = result[:, 2:3]
 
         def combine(t):
             scaled_ih, scaled_hh = scaled[t]
-            nc.vector.scalar_tensor_tensor(
-                out=scaled_hh[:],
-                in0=scaled_hh[:],
-                scalar=rstd[t][:, 1:2],
-                in1=beta_sum[:],
-                op0=ALU.mult,
-                op1=ALU.add,
-            )
-            nc.vector.scalar_tensor_tensor(
-                out=scaled_ih[:],
-                in0=scaled_ih[:],
-                scalar=rstd[t][:, 0:1],
-                in1=scaled_hh[:],
-                op0=ALU.mult,
-                op1=ALU.add,
-            )
+            for half in range(2):
+                cols = slice(half * 2 * H, (half + 1) * 2 * H)
+                nc.vector.scalar_tensor_tensor(
+                    out=scaled_hh[:, cols],
+                    in0=scaled_hh[:, cols],
+                    scalar=rstd[t][:, 1:2],
+                    in1=beta_sum[:, cols],
+                    op0=ALU.mult,
+                    op1=ALU.add,
+                )
+                nc.vector.scalar_tensor_tensor(
+                    out=scaled_ih[:, cols],
+                    in0=scaled_ih[:, cols],
+                    scalar=rstd[t][:, 0:1],
+                    in1=scaled_hh[:, cols],
+                    op0=ALU.mult,
+                    op1=ALU.add,
+                )
 
         def gate_functions(t):
             gates = scaled[t][0]
@@ -287,16 +310,15 @@ def tile_layernormlstmcell_kernel(
                 scale=-1.0 / H,
                 accum_out=neg_mean_c[t][:],
             )
-            sq_sum = stats.tile([P, 1], F32, name="sq_sum_c")
+            sq_sum_c[t] = stats.tile([P, 1], F32, name="sq_sum_c")
             scrap = stage.tile([P, BANK], BF16, name="scrap")
             nc.scalar.activation(
                 out=scrap[:],
                 in_=c_new[t][:],
                 func=ACT.Square,
                 bias=neg_mean_c[t][:],
-                accum_out=sq_sum[:],
+                accum_out=sq_sum_c[t][:],
             )
-            rstd_c[t] = inverse_std(sq_sum[:], H, 1)
 
         def cell_norm(t):
             normed[t] = narrow.tile([P, H], F32, name="normed")
@@ -311,7 +333,7 @@ def tile_layernormlstmcell_kernel(
             nc.vector.scalar_tensor_tensor(
                 out=normed[t][:],
                 in0=normed[t][:],
-                scalar=rstd_c[t][:],
+                scalar=rstd_c[t],
                 in1=beta_c_sb[:],
                 op0=ALU.mult,
                 op1=ALU.add,
@@ -322,7 +344,7 @@ def tile_layernormlstmcell_kernel(
 
         def hidden_out(t):
             h_new = narrow.tile([P, H], F32)
-            nc.gpsimd.tensor_tensor(out=h_new[:], in0=o_gate[t][:], in1=normed[t][:], op=ALU.mult)
+            nc.vector.tensor_tensor(out=h_new[:], in0=o_gate[t][:], in1=normed[t][:], op=ALU.mult)
             nc.sync.dma_start(out=h_out[:, t, :], in_=h_new[:])
 
         def on(stage_of, t):
@@ -330,16 +352,16 @@ def tile_layernormlstmcell_kernel(
                 stage_of(t)
 
         with tc.manual_schedule():
-            for i in range(-2, ROW_TILES + 3):
-                on(gate_rstd, i - 1)
-                on(cell_norm, i - 3)
+            for i in range(-3, ROW_TILES + 4):
+                inverse_stds(i - 1, i - 3)
                 on(gate_functions, i - 2)
-                on(cell_tanh, i - 3)
-                on(flip_rows, i + 2)
-                on(row_means, i + 1)
                 on(products, i)
+                on(cell_state, i - 2)
+                on(cell_norm, i - 3)
+                on(hidden_out, i - 4)
                 on(quantise_rows, i + 2)
                 on(combine, i - 1)
-                on(cell_state, i - 2)
-                on(hidden_out, i - 3)
                 on(cell_stats, i - 2)
+                on(cell_tanh, i - 3)
+                on(flip_rows, i + 3)
+                on(row_means, i + 1)

@@ -134,6 +134,7 @@ def tile_layernormlstmcell_kernel(
         rows_mx = {}
         neg_mean = {}
         sq_part = {}
+        sq_sum = {}
         scaled = {}
         rstd = {}
         o_gate = {}
@@ -221,6 +222,10 @@ def tile_layernormlstmcell_kernel(
                         accum_out=sq_part[t][:, s, j : j + 1],
                     )
 
+        def sum_squares(t):
+            sq_sum[t] = stats.tile([P, 2], F32, name="sq_sum")
+            nc.vector.tensor_reduce(out=sq_sum[t][:], in_=sq_part[t][:], axis=AX.X, op=ALU.add)
+
         def inverse_stds(gate_tile, cell_tile):
             gates_live = 0 <= gate_tile < ROW_TILES
             cell_live = 0 <= cell_tile < ROW_TILES
@@ -228,13 +233,9 @@ def tile_layernormlstmcell_kernel(
                 return
             var = stats.tile([P, 3], F32)
             if gates_live:
-                sq_sum = stats.tile([P, 2], F32)
-                nc.vector.tensor_reduce(
-                    out=sq_sum[:], in_=sq_part[gate_tile][:], axis=AX.X, op=ALU.add
-                )
                 nc.vector.tensor_scalar(
                     out=var[:, 0:2],
-                    in0=sq_sum[:],
+                    in0=sq_sum[gate_tile][:],
                     scalar1=1.0 / G,
                     scalar2=EPS,
                     op0=ALU.mult,
@@ -257,26 +258,28 @@ def tile_layernormlstmcell_kernel(
             rstd[gate_tile] = result[:, 0:2]
             rstd_c[cell_tile] = result[:, 2:3]
 
-        def combine(t):
+        def shift_hh(t):
+            scaled_hh = scaled[t][1]
+            nc.vector.scalar_tensor_tensor(
+                out=scaled_hh[:],
+                in0=scaled_hh[:],
+                scalar=rstd[t][:, 1:2],
+                in1=beta_sum[:],
+                op0=ALU.mult,
+                op1=ALU.add,
+            )
+
+        def add_ih(t, half):
             scaled_ih, scaled_hh = scaled[t]
-            for half in range(2):
-                cols = slice(half * 2 * H, (half + 1) * 2 * H)
-                nc.vector.scalar_tensor_tensor(
-                    out=scaled_hh[:, cols],
-                    in0=scaled_hh[:, cols],
-                    scalar=rstd[t][:, 1:2],
-                    in1=beta_sum[:, cols],
-                    op0=ALU.mult,
-                    op1=ALU.add,
-                )
-                nc.vector.scalar_tensor_tensor(
-                    out=scaled_ih[:, cols],
-                    in0=scaled_ih[:, cols],
-                    scalar=rstd[t][:, 0:1],
-                    in1=scaled_hh[:, cols],
-                    op0=ALU.mult,
-                    op1=ALU.add,
-                )
+            cols = slice(half * 2 * H, (half + 1) * 2 * H)
+            nc.vector.scalar_tensor_tensor(
+                out=scaled_ih[:, cols],
+                in0=scaled_ih[:, cols],
+                scalar=rstd[t][:, 0:1],
+                in1=scaled_hh[:, cols],
+                op0=ALU.mult,
+                op1=ALU.add,
+            )
 
         def gate_functions(t):
             gates = scaled[t][0]
@@ -300,7 +303,7 @@ def tile_layernormlstmcell_kernel(
             nc.gpsimd.tensor_tensor(out=c_new[t][:], in0=c_new[t][:], in1=kept[:], op=ALU.add)
             nc.sync.dma_start(out=c_out[:, t, :], in_=c_new[t][:])
 
-        def cell_stats(t):
+        def cell_mean(t):
             neg_mean_c[t] = stats.tile([P, 1], F32, name="neg_mean_c")
             scrap = stage.tile([P, BANK], BF16, name="scrap")
             nc.scalar.activation(
@@ -310,6 +313,8 @@ def tile_layernormlstmcell_kernel(
                 scale=-1.0 / H,
                 accum_out=neg_mean_c[t][:],
             )
+
+        def cell_squares(t):
             sq_sum_c[t] = stats.tile([P, 1], F32, name="sq_sum_c")
             scrap = stage.tile([P, BANK], BF16, name="scrap")
             nc.scalar.activation(
@@ -320,7 +325,7 @@ def tile_layernormlstmcell_kernel(
                 accum_out=sq_sum_c[t][:],
             )
 
-        def cell_norm(t):
+        def cell_centre(t):
             normed[t] = narrow.tile([P, H], F32, name="normed")
             nc.vector.scalar_tensor_tensor(
                 out=normed[t][:],
@@ -330,6 +335,8 @@ def tile_layernormlstmcell_kernel(
                 op0=ALU.add,
                 op1=ALU.mult,
             )
+
+        def cell_scale(t):
             nc.vector.scalar_tensor_tensor(
                 out=normed[t][:],
                 in0=normed[t][:],
@@ -347,21 +354,26 @@ def tile_layernormlstmcell_kernel(
             nc.vector.tensor_tensor(out=h_new[:], in0=o_gate[t][:], in1=normed[t][:], op=ALU.mult)
             nc.sync.dma_start(out=h_out[:, t, :], in_=h_new[:])
 
-        def on(stage_of, t):
+        def on(stage_of, t, *more):
             if 0 <= t < ROW_TILES:
-                stage_of(t)
+                stage_of(t, *more)
 
         with tc.manual_schedule():
             for i in range(-3, ROW_TILES + 4):
-                inverse_stds(i - 1, i - 3)
                 on(gate_functions, i - 2)
                 on(products, i)
                 on(cell_state, i - 2)
-                on(cell_norm, i - 3)
+                on(cell_centre, i - 3)
                 on(hidden_out, i - 4)
-                on(quantise_rows, i + 2)
-                on(combine, i - 1)
-                on(cell_stats, i - 2)
+                on(cell_scale, i - 3)
+                on(cell_mean, i - 2)
                 on(cell_tanh, i - 3)
+                on(cell_squares, i - 2)
+                on(shift_hh, i - 1)
+                on(quantise_rows, i + 2)
+                on(add_ih, i - 1, 0)
+                on(sum_squares, i)
+                on(add_ih, i - 1, 1)
+                inverse_stds(i, i - 2)
                 on(flip_rows, i + 3)
                 on(row_means, i + 1)

@@ -71,8 +71,13 @@ def tile_layernormlstmcell_kernel(
 
         minus_half = const.tile([P, 3], F32)
         nc.vector.memset(minus_half[:], -0.5)
-        ident = const.tile([P, P], F32)
-        make_identity(nc, ident[:])
+
+        gain_rows = const.tile([P, 2, G], BF16)
+        shift_rows = const.tile([P, G], BF16)
+        cell_rows = const.tile([P, 2, H], BF16)
+        nc.vector.memset(gain_rows[:].bitcast(I32), 0)
+        nc.scalar.dma_start(out=gain_rows[0:1, 0, :], in_=gamma_ih.unsqueeze(0))
+        nc.scalar.dma_start(out=gain_rows[0:1, 1, :], in_=gamma_hh.unsqueeze(0))
 
         w_scales = [
             const.tile([P, G], U8, name="w_ih_scales", align_bytes=64),
@@ -81,28 +86,39 @@ def tile_layernormlstmcell_kernel(
         for plane in w_scales:
             nc.vector.memset(plane[:].bitcast(I32), 0)
 
+        nc.vector.memset(shift_rows[:].bitcast(I32), 0)
+        nc.scalar.dma_start(out=shift_rows[0:1, :], in_=beta_ih.unsqueeze(0))
+        nc.scalar.dma_start(out=shift_rows[1:2, :], in_=beta_hh.unsqueeze(0))
+        nc.vector.memset(cell_rows[:].bitcast(I32), 0)
+        nc.scalar.dma_start(out=cell_rows[0:1, 0, :], in_=gamma_c.unsqueeze(0))
+        nc.scalar.dma_start(out=cell_rows[0:1, 1, :], in_=beta_c.unsqueeze(0))
+
+        ones = const.tile([P, P], BF16)
+        nc.vector.memset(ones[:], 1.0)
+        ident = const.tile([P, P], F32)
+        make_identity(nc, ident[:])
+
         x_sb = const.tile([P, ROW_TILES, K], BF16)
         h_sb = const.tile([P, ROW_TILES, K], BF16)
         c_sb = const.tile([P, ROW_TILES, H], BF16)
         first = slice(0, LOAD_TILES)
         nc.sync.dma_start(out=x_sb[:, first, :], in_=x_rows[:, first, :])
         nc.sync.dma_start(out=h_sb[:, first, :], in_=h_rows[:, first, :])
-
-        for plane, rows in zip(w_scales, (W_ih_scales[0], W_hh_scales[0])):
-            for quad in range(4):
-                nc.sync.dma_start(
-                    out=plane[32 * quad : 32 * quad + 4, :].bitcast(I32),
-                    in_=rows[4 * quad : 4 * quad + 4, :].bitcast(I32),
-                )
-
         w_words = [
             const.tile([P, 4 * G], U8, name="w_ih_words", align_bytes=64),
             const.tile([P, 4 * G], U8, name="w_hh_words", align_bytes=64),
         ]
-        for words, source in zip(w_words, (W_ih_words[0], W_hh_words[0])):
+        for s, (words, rows) in enumerate(
+            ((W_ih_words[0], W_ih_scales[0]), (W_hh_words[0], W_hh_scales[0]))
+        ):
+            for quad in range(4):
+                nc.sync.dma_start(
+                    out=w_scales[s][32 * quad : 32 * quad + 4, :].bitcast(I32),
+                    in_=rows[4 * quad : 4 * quad + 4, :].bitcast(I32),
+                )
             nc.sync.dma_start(
-                out=words[:].bitcast(I32),
-                in_=source.rearrange("p n t -> p (n t)").bitcast(I32),
+                out=w_words[s][:].bitcast(I32),
+                in_=words.rearrange("p n t -> p (n t)").bitcast(I32),
             )
         nc.sync.dma_start(out=c_sb[:, first, :], in_=c_rows[:, first, :])
         for start in range(LOAD_TILES, ROW_TILES, LOAD_TILES):
@@ -115,20 +131,17 @@ def tile_layernormlstmcell_kernel(
             const.tile([P, G], BF16, name="gamma_ih_sb"),
             const.tile([P, G], BF16, name="gamma_hh_sb"),
         ]
-        nc.scalar.dma_start(out=gamma[0][:], in_=gamma_ih.partition_broadcast(P))
-        nc.scalar.dma_start(out=gamma[1][:], in_=gamma_hh.partition_broadcast(P))
-        beta_ih_sb = const.tile([P, G], BF16)
-        beta_hh_sb = const.tile([P, G], BF16)
-        nc.scalar.dma_start(out=beta_ih_sb[:], in_=beta_ih.partition_broadcast(P))
-        nc.scalar.dma_start(out=beta_hh_sb[:], in_=beta_hh.partition_broadcast(P))
-        gamma_c_sb = const.tile([P, H], BF16)
-        beta_c_sb = const.tile([P, H], BF16)
-        nc.scalar.dma_start(out=gamma_c_sb[:], in_=gamma_c.partition_broadcast(P))
-        nc.scalar.dma_start(out=beta_c_sb[:], in_=beta_c.partition_broadcast(P))
         beta_sum = const.tile([P, G], F32)
-        nc.gpsimd.tensor_tensor(
-            out=beta_sum[:], in0=beta_ih_sb[:], in1=beta_hh_sb[:], op=ALU.add
-        )
+        cell_vectors = const.tile([P, 2, H], BF16)
+        gamma_c_sb = cell_vectors[:, 0, :]
+        beta_c_sb = cell_vectors[:, 1, :]
+
+        def spread(rows, out):
+            for j in range(rows.shape[1] // BANK):
+                cols = slice(j * BANK, (j + 1) * BANK)
+                acc = psum_acc.tile([P, BANK], F32)
+                nc.tensor.matmul(out=acc[:], lhsT=ones[:], rhs=rows[:, cols], start=True, stop=True)
+                nc.scalar.copy(out=out[:, cols], in_=acc[:])
 
         grouped = {}
         rows_mx = {}
@@ -331,7 +344,7 @@ def tile_layernormlstmcell_kernel(
                 out=normed[t][:],
                 in0=c_new[t][:],
                 scalar=neg_mean_c[t][:],
-                in1=gamma_c_sb[:],
+                in1=gamma_c_sb,
                 op0=ALU.add,
                 op1=ALU.mult,
             )
@@ -341,7 +354,7 @@ def tile_layernormlstmcell_kernel(
                 out=normed[t][:],
                 in0=normed[t][:],
                 scalar=rstd_c[t],
-                in1=beta_c_sb[:],
+                in1=beta_c_sb,
                 op0=ALU.mult,
                 op1=ALU.add,
             )
@@ -358,22 +371,31 @@ def tile_layernormlstmcell_kernel(
             if 0 <= t < ROW_TILES:
                 stage_of(t, *more)
 
+        def round_of(i):
+            on(gate_functions, i - 2)
+            on(products, i)
+            on(cell_state, i - 2)
+            on(cell_centre, i - 3)
+            on(hidden_out, i - 4)
+            on(cell_scale, i - 3)
+            on(cell_mean, i - 2)
+            on(cell_tanh, i - 3)
+            on(cell_squares, i - 2)
+            on(shift_hh, i - 1)
+            on(quantise_rows, i + 2)
+            on(add_ih, i - 1, 0)
+            on(sum_squares, i)
+            on(add_ih, i - 1, 1)
+            inverse_stds(i, i - 2)
+            on(flip_rows, i + 3)
+            on(row_means, i + 1)
+
         with tc.manual_schedule():
-            for i in range(-3, ROW_TILES + 4):
-                on(gate_functions, i - 2)
-                on(products, i)
-                on(cell_state, i - 2)
-                on(cell_centre, i - 3)
-                on(hidden_out, i - 4)
-                on(cell_scale, i - 3)
-                on(cell_mean, i - 2)
-                on(cell_tanh, i - 3)
-                on(cell_squares, i - 2)
-                on(shift_hh, i - 1)
-                on(quantise_rows, i + 2)
-                on(add_ih, i - 1, 0)
-                on(sum_squares, i)
-                on(add_ih, i - 1, 1)
-                inverse_stds(i, i - 2)
-                on(flip_rows, i + 3)
-                on(row_means, i + 1)
+            spread(gain_rows[:, 0, :], gamma[0])
+            spread(gain_rows[:, 1, :], gamma[1])
+            for i in range(-3, 1):
+                round_of(i)
+            spread(shift_rows[:], beta_sum)
+            spread(cell_rows[:].rearrange("p v h -> p (v h)"), cell_vectors[:].rearrange("p v h -> p (v h)"))
+            for i in range(1, ROW_TILES + 4):
+                round_of(i)

@@ -52,11 +52,13 @@ def tile_layernormlstmcell_kernel(
         stage = ctx.enter_context(tc.tile_pool(name="stage", bufs=2))
         operand = ctx.enter_context(tc.tile_pool(name="operand", bufs=4))
         stats = ctx.enter_context(tc.tile_pool(name="stats", bufs=4))
-        wide = ctx.enter_context(tc.tile_pool(name="wide", bufs=3))
-        narrow = ctx.enter_context(tc.tile_pool(name="narrow", bufs=3))
+        wide_ih = ctx.enter_context(tc.tile_pool(name="wide_ih", bufs=4))
+        wide_hh = ctx.enter_context(tc.tile_pool(name="wide_hh", bufs=2))
+        narrow = ctx.enter_context(tc.tile_pool(name="narrow", bufs=4))
         psum_flip = ctx.enter_context(tc.psum_pool(name="psum_flip", bufs=1))
         psum_fold = ctx.enter_context(tc.psum_pool(name="psum_fold", bufs=1))
-        psum_acc = ctx.enter_context(tc.psum_pool(name="psum_acc", bufs=6))
+        psum_cell = ctx.enter_context(tc.psum_pool(name="psum_cell", bufs=1))
+        psum_acc = ctx.enter_context(tc.psum_pool(name="psum_acc", bufs=5))
 
         x_rows = x.rearrange("(p t) k -> p t k", t=ROW_TILES)
         h_rows = h_prev.rearrange("(p t) k -> p t k", t=ROW_TILES)
@@ -132,9 +134,9 @@ def tile_layernormlstmcell_kernel(
             const.tile([P, G], BF16, name="gamma_hh_sb"),
         ]
         beta_sum = const.tile([P, G], F32)
-        cell_vectors = const.tile([P, 2, H], BF16)
-        gamma_c_sb = cell_vectors[:, 0, :]
-        beta_c_sb = cell_vectors[:, 1, :]
+        cell_vectors = psum_cell.tile([P, 2, H], BF16)
+        gamma_c_ps = cell_vectors[:, 0, :]
+        beta_c_ps = cell_vectors[:, 1, :]
 
         def spread(rows, out):
             for j in range(rows.shape[1] // BANK):
@@ -148,6 +150,8 @@ def tile_layernormlstmcell_kernel(
         neg_mean = {}
         sq_part = {}
         sq_sum = {}
+        var = {}
+        kept = {}
         scaled = {}
         rstd = {}
         o_gate = {}
@@ -210,8 +214,8 @@ def tile_layernormlstmcell_kernel(
         def products(t):
             sq_part[t] = stats.tile([P, 2, BANKS], F32, name="sq_part")
             scaled[t] = (
-                wide.tile([P, G], F32, name="scaled_ih"),
-                wide.tile([P, G], F32, name="scaled_hh"),
+                wide_ih.tile([P, G], F32, name="scaled_ih"),
+                wide_hh.tile([P, G], F32, name="scaled_hh"),
             )
             for s in range(2):
                 for j in range(BANKS):
@@ -239,34 +243,46 @@ def tile_layernormlstmcell_kernel(
             sq_sum[t] = stats.tile([P, 2], F32, name="sq_sum")
             nc.vector.tensor_reduce(out=sq_sum[t][:], in_=sq_part[t][:], axis=AX.X, op=ALU.add)
 
-        def inverse_stds(gate_tile, cell_tile):
-            gates_live = 0 <= gate_tile < ROW_TILES
-            cell_live = 0 <= cell_tile < ROW_TILES
-            if not (gates_live or cell_live):
+        def live_columns(gate_tile, cell_tile):
+            first_col = 0 if 0 <= gate_tile < ROW_TILES else 2
+            end_col = 3 if 0 <= cell_tile < ROW_TILES else 2
+            return first_col, end_col
+
+        def variances(gate_tile, cell_tile):
+            first_col, end_col = live_columns(gate_tile, cell_tile)
+            if first_col == end_col:
                 return
-            var = stats.tile([P, 3], F32)
-            if gates_live:
+            var[gate_tile] = stats.tile([P, 3], F32, name="var")
+            if first_col == 0:
                 nc.vector.tensor_scalar(
-                    out=var[:, 0:2],
+                    out=var[gate_tile][:, 0:2],
                     in0=sq_sum[gate_tile][:],
                     scalar1=1.0 / G,
                     scalar2=EPS,
                     op0=ALU.mult,
                     op1=ALU.add,
                 )
-            if cell_live:
+            if end_col == 3:
                 nc.vector.tensor_scalar(
-                    out=var[:, 2:3],
+                    out=var[gate_tile][:, 2:3],
                     in0=sq_sum_c[cell_tile][:],
                     scalar1=1.0 / H,
                     scalar2=EPS,
                     op0=ALU.mult,
                     op1=ALU.add,
                 )
-            live = slice(0 if gates_live else 2, 3 if cell_live else 2)
+
+        def inverse_roots(gate_tile, cell_tile):
+            first_col, end_col = live_columns(gate_tile, cell_tile)
+            if first_col == end_col:
+                return
+            live = slice(first_col, end_col)
             result = stats.tile([P, 3], F32)
             nc.gpsimd.tensor_tensor(
-                out=result[:, live], in0=var[:, live], in1=minus_half[:, live], op=ALU.pow
+                out=result[:, live],
+                in0=var[gate_tile][:, live],
+                in1=minus_half[:, live],
+                op=ALU.pow,
             )
             rstd[gate_tile] = result[:, 0:2]
             rstd_c[cell_tile] = result[:, 2:3]
@@ -300,20 +316,26 @@ def tile_layernormlstmcell_kernel(
             nc.scalar.activation(
                 out=gates[:, 2 * H : 3 * H], in_=gates[:, 2 * H : 3 * H], func=ACT.Tanh
             )
-            o_gate[t] = narrow.tile([P, H], F32, name="o_gate")
-            nc.scalar.activation(out=o_gate[t][:], in_=gates[:, 3 * H : 4 * H], func=ACT.Sigmoid)
 
-        def cell_state(t):
+        def output_gate(t):
+            o_gate[t] = narrow.tile([P, H], F32, name="o_gate")
+            nc.scalar.activation(
+                out=o_gate[t][:], in_=scaled[t][0][:, 3 * H : 4 * H], func=ACT.Sigmoid
+            )
+
+        def cell_products(t):
             gates = scaled[t][0]
-            kept = narrow.tile([P, H], F32)
+            kept[t] = narrow.tile([P, H], F32, name="kept")
             nc.gpsimd.tensor_tensor(
-                out=kept[:], in0=gates[:, H : 2 * H], in1=c_sb[:, t, :], op=ALU.mult
+                out=kept[t][:], in0=gates[:, H : 2 * H], in1=c_sb[:, t, :], op=ALU.mult
             )
             c_new[t] = narrow.tile([P, H], F32, name="c_new")
             nc.gpsimd.tensor_tensor(
                 out=c_new[t][:], in0=gates[:, 0:H], in1=gates[:, 2 * H : 3 * H], op=ALU.mult
             )
-            nc.gpsimd.tensor_tensor(out=c_new[t][:], in0=c_new[t][:], in1=kept[:], op=ALU.add)
+
+        def cell_sum(t):
+            nc.gpsimd.tensor_tensor(out=c_new[t][:], in0=c_new[t][:], in1=kept[t][:], op=ALU.add)
             nc.sync.dma_start(out=c_out[:, t, :], in_=c_new[t][:])
 
         def cell_mean(t):
@@ -344,7 +366,7 @@ def tile_layernormlstmcell_kernel(
                 out=normed[t][:],
                 in0=c_new[t][:],
                 scalar=neg_mean_c[t][:],
-                in1=gamma_c_sb,
+                in1=gamma_c_ps,
                 op0=ALU.add,
                 op1=ALU.mult,
             )
@@ -354,7 +376,7 @@ def tile_layernormlstmcell_kernel(
                 out=normed[t][:],
                 in0=normed[t][:],
                 scalar=rstd_c[t],
-                in1=beta_c_sb,
+                in1=beta_c_ps,
                 op0=ALU.mult,
                 op1=ALU.add,
             )
@@ -373,20 +395,23 @@ def tile_layernormlstmcell_kernel(
 
         def round_of(i):
             on(gate_functions, i - 2)
+            on(cell_products, i - 3)
+            inverse_roots(i - 1, i - 4)
+            on(cell_sum, i - 3)
+            on(cell_centre, i - 4)
             on(products, i)
-            on(cell_state, i - 2)
-            on(cell_centre, i - 3)
-            on(hidden_out, i - 4)
-            on(cell_scale, i - 3)
-            on(cell_mean, i - 2)
-            on(cell_tanh, i - 3)
-            on(cell_squares, i - 2)
+            on(cell_scale, i - 4)
+            on(hidden_out, i - 5)
+            on(output_gate, i - 2)
+            on(cell_mean, i - 3)
+            on(cell_tanh, i - 4)
+            on(cell_squares, i - 3)
             on(shift_hh, i - 1)
             on(quantise_rows, i + 2)
             on(add_ih, i - 1, 0)
             on(sum_squares, i)
             on(add_ih, i - 1, 1)
-            inverse_stds(i, i - 2)
+            variances(i, i - 3)
             on(flip_rows, i + 3)
             on(row_means, i + 1)
 
@@ -396,6 +421,9 @@ def tile_layernormlstmcell_kernel(
             for i in range(-3, 1):
                 round_of(i)
             spread(shift_rows[:], beta_sum)
-            spread(cell_rows[:].rearrange("p v h -> p (v h)"), cell_vectors[:].rearrange("p v h -> p (v h)"))
-            for i in range(1, ROW_TILES + 4):
+            for v in range(2):
+                nc.tensor.matmul(
+                    out=cell_vectors[:, v, :], lhsT=ones[:], rhs=cell_rows[:, v, :], start=True, stop=True
+                )
+            for i in range(1, ROW_TILES + 5):
                 round_of(i)

@@ -24,6 +24,7 @@ BANK = 512
 BANKS = G // BANK
 FOLD = 128
 LOAD_TILES = 4
+FIRST_TILES = 2
 
 FLOPS = 2 * 2 * B * K * G
 
@@ -71,39 +72,30 @@ def tile_layernormlstmcell_kernel(
         warm = const.tile([P, 1], F32)
         nc.scalar.activation(out=warm[:], in_=zero[:], func=ACT.Sigmoid)
 
-        minus_half = const.tile([P, 3], F32)
-        nc.vector.memset(minus_half[:], -0.5)
-
-        gain_rows = const.tile([P, 2, G], BF16)
-        shift_rows = const.tile([P, G], BF16)
-        cell_rows = const.tile([P, 2, H], BF16)
-        nc.vector.memset(gain_rows[:].bitcast(I32), 0)
-        nc.scalar.dma_start(out=gain_rows[0:1, 0, :], in_=gamma_ih.unsqueeze(0))
-        nc.scalar.dma_start(out=gain_rows[0:1, 1, :], in_=gamma_hh.unsqueeze(0))
-
+        vector_rows = const.tile([P, G], BF16)
+        nc.vector.memset(vector_rows[:].bitcast(I32), 0)
+        for row, vector in enumerate((gamma_ih, gamma_hh, beta_ih, beta_hh, gamma_c, beta_c)):
+            nc.scalar.dma_start(
+                out=vector_rows[row : row + 1, 0 : vector.shape[0]], in_=vector.unsqueeze(0)
+            )
         w_scales = [
             const.tile([P, G], U8, name="w_ih_scales", align_bytes=64),
             const.tile([P, G], U8, name="w_hh_scales", align_bytes=64),
         ]
         for plane in w_scales:
             nc.vector.memset(plane[:].bitcast(I32), 0)
-
-        nc.vector.memset(shift_rows[:].bitcast(I32), 0)
-        nc.scalar.dma_start(out=shift_rows[0:1, :], in_=beta_ih.unsqueeze(0))
-        nc.scalar.dma_start(out=shift_rows[1:2, :], in_=beta_hh.unsqueeze(0))
-        nc.vector.memset(cell_rows[:].bitcast(I32), 0)
-        nc.scalar.dma_start(out=cell_rows[0:1, 0, :], in_=gamma_c.unsqueeze(0))
-        nc.scalar.dma_start(out=cell_rows[0:1, 1, :], in_=beta_c.unsqueeze(0))
-
-        ones = const.tile([P, P], BF16)
-        nc.vector.memset(ones[:], 1.0)
+        minus_half = const.tile([P, 3], F32)
+        nc.vector.memset(minus_half[:], -0.5)
         ident = const.tile([P, P], F32)
         make_identity(nc, ident[:])
+        pick = const.tile([P, 6], BF16)
+        nc.scalar.copy(out=pick[:], in_=ident[:, 0:6])
+        nc.vector.tensor_tensor(out=pick[:, 2:3], in0=ident[:, 2:3], in1=ident[:, 3:4], op=ALU.add)
 
         x_sb = const.tile([P, ROW_TILES, K], BF16)
         h_sb = const.tile([P, ROW_TILES, K], BF16)
         c_sb = const.tile([P, ROW_TILES, H], BF16)
-        first = slice(0, LOAD_TILES)
+        first = slice(0, FIRST_TILES)
         nc.sync.dma_start(out=x_sb[:, first, :], in_=x_rows[:, first, :])
         nc.sync.dma_start(out=h_sb[:, first, :], in_=h_rows[:, first, :])
         w_words = [
@@ -122,7 +114,10 @@ def tile_layernormlstmcell_kernel(
                 out=w_words[s][:].bitcast(I32),
                 in_=words.rearrange("p n t -> p (n t)").bitcast(I32),
             )
-        nc.sync.dma_start(out=c_sb[:, first, :], in_=c_rows[:, first, :])
+        second = slice(FIRST_TILES, LOAD_TILES)
+        nc.sync.dma_start(out=x_sb[:, second, :], in_=x_rows[:, second, :])
+        nc.sync.dma_start(out=h_sb[:, second, :], in_=h_rows[:, second, :])
+        nc.sync.dma_start(out=c_sb[:, 0:LOAD_TILES, :], in_=c_rows[:, 0:LOAD_TILES, :])
         for start in range(LOAD_TILES, ROW_TILES, LOAD_TILES):
             chunk = slice(start, start + LOAD_TILES)
             nc.sync.dma_start(out=x_sb[:, chunk, :], in_=x_rows[:, chunk, :])
@@ -138,14 +133,27 @@ def tile_layernormlstmcell_kernel(
         gamma_c_ps = cell_vectors[:, 0, :]
         beta_c_ps = cell_vectors[:, 1, :]
 
-        def spread(rows, out):
-            for j in range(rows.shape[1] // BANK):
+        def spread_bank(acc, r, cols):
+            nc.tensor.matmul(
+                out=acc,
+                lhsT=pick[:, r : r + 1].to_broadcast([P, P]),
+                rhs=vector_rows[:, cols],
+                start=True,
+                stop=True,
+            )
+
+        def spread(r, out):
+            for j in range(BANKS):
                 cols = slice(j * BANK, (j + 1) * BANK)
-                acc = psum_acc.tile([P, BANK], F32)
-                nc.tensor.matmul(out=acc[:], lhsT=ones[:], rhs=rows[:, cols], start=True, stop=True)
-                nc.scalar.copy(out=out[:, cols], in_=acc[:])
+                acc = psum_acc.tile([P, BANK], F32, name="acc")
+                spread_bank(acc[:], r, cols)
+                if j % 2 == 0:
+                    nc.scalar.copy(out=out[:, cols], in_=acc[:])
+                else:
+                    nc.vector.tensor_copy(out=out[:, cols], in_=acc[:])
 
         grouped = {}
+        fold = {}
         rows_mx = {}
         neg_mean = {}
         sq_part = {}
@@ -195,49 +203,61 @@ def tile_layernormlstmcell_kernel(
                 stop=stop,
             )
 
+        def fold_passes(t, s):
+            if s == 0:
+                fold[t] = psum_fold.tile([P, 2, FOLD], F32, name="fold")
+            for j in range(G // FOLD):
+                mx_pass(fold[t][:, s, :], t, s, j * FOLD, FOLD, j == 0, j == G // FOLD - 1)
+
+        def fold_sum(t, s):
+            if s == 0:
+                neg_mean[t] = stats.tile([P, 2], F32, name="neg_mean")
+            scrap = stage.tile([P, BANK], BF16, name="scrap")
+            nc.scalar.activation(
+                out=scrap[:, 0:FOLD],
+                in_=fold[t][:, s, :],
+                func=ACT.Copy,
+                scale=-1.0 / G,
+                accum_out=neg_mean[t][:, s : s + 1],
+            )
+
         def row_means(t):
-            fold = psum_fold.tile([P, 2, FOLD], F32)
             for s in range(2):
-                for j in range(G // FOLD):
-                    mx_pass(fold[:, s, :], t, s, j * FOLD, FOLD, j == 0, j == G // FOLD - 1)
-            neg_mean[t] = stats.tile([P, 2], F32, name="neg_mean")
+                fold_passes(t, s)
             for s in range(2):
+                fold_sum(t, s)
+
+        def product(t, s):
+            if s == 0:
+                sq_part[t] = stats.tile([P, 2, BANKS], F32, name="sq_part")
+                scaled[t] = (
+                    wide_ih.tile([P, G], F32, name="scaled_ih"),
+                    wide_hh.tile([P, G], F32, name="scaled_hh"),
+                )
+            for j in range(BANKS):
+                cols = slice(j * BANK, (j + 1) * BANK)
+                acc = psum_acc.tile([P, BANK], F32, name="acc")
+                mx_pass(acc[:], t, s, j * BANK, BANK, True, True)
+                nc.vector.scalar_tensor_tensor(
+                    out=scaled[t][s][:, cols],
+                    in0=acc[:],
+                    scalar=neg_mean[t][:, s : s + 1],
+                    in1=gamma[s][:, cols],
+                    op0=ALU.add,
+                    op1=ALU.mult,
+                )
                 scrap = stage.tile([P, BANK], BF16, name="scrap")
                 nc.scalar.activation(
-                    out=scrap[:, 0:FOLD],
-                    in_=fold[:, s, :],
-                    func=ACT.Copy,
-                    scale=-1.0 / G,
-                    accum_out=neg_mean[t][:, s : s + 1],
+                    out=scrap[:],
+                    in_=acc[:],
+                    func=ACT.Square,
+                    bias=neg_mean[t][:, s : s + 1],
+                    accum_out=sq_part[t][:, s, j : j + 1],
                 )
 
         def products(t):
-            sq_part[t] = stats.tile([P, 2, BANKS], F32, name="sq_part")
-            scaled[t] = (
-                wide_ih.tile([P, G], F32, name="scaled_ih"),
-                wide_hh.tile([P, G], F32, name="scaled_hh"),
-            )
-            for s in range(2):
-                for j in range(BANKS):
-                    cols = slice(j * BANK, (j + 1) * BANK)
-                    acc = psum_acc.tile([P, BANK], F32)
-                    mx_pass(acc[:], t, s, j * BANK, BANK, True, True)
-                    nc.vector.scalar_tensor_tensor(
-                        out=scaled[t][s][:, cols],
-                        in0=acc[:],
-                        scalar=neg_mean[t][:, s : s + 1],
-                        in1=gamma[s][:, cols],
-                        op0=ALU.add,
-                        op1=ALU.mult,
-                    )
-                    scrap = stage.tile([P, BANK], BF16, name="scrap")
-                    nc.scalar.activation(
-                        out=scrap[:],
-                        in_=acc[:],
-                        func=ACT.Square,
-                        bias=neg_mean[t][:, s : s + 1],
-                        accum_out=sq_part[t][:, s, j : j + 1],
-                    )
+            product(t, 0)
+            product(t, 1)
 
         def sum_squares(t):
             sq_sum[t] = stats.tile([P, 2], F32, name="sq_sum")
@@ -323,19 +343,19 @@ def tile_layernormlstmcell_kernel(
                 out=o_gate[t][:], in_=scaled[t][0][:, 3 * H : 4 * H], func=ACT.Sigmoid
             )
 
-        def cell_products(t):
+        def cell_products(t, engine=nc.gpsimd):
             gates = scaled[t][0]
             kept[t] = narrow.tile([P, H], F32, name="kept")
-            nc.gpsimd.tensor_tensor(
+            engine.tensor_tensor(
                 out=kept[t][:], in0=gates[:, H : 2 * H], in1=c_sb[:, t, :], op=ALU.mult
             )
             c_new[t] = narrow.tile([P, H], F32, name="c_new")
-            nc.gpsimd.tensor_tensor(
+            engine.tensor_tensor(
                 out=c_new[t][:], in0=gates[:, 0:H], in1=gates[:, 2 * H : 3 * H], op=ALU.mult
             )
 
-        def cell_sum(t):
-            nc.gpsimd.tensor_tensor(out=c_new[t][:], in0=c_new[t][:], in1=kept[t][:], op=ALU.add)
+        def cell_sum(t, engine=nc.gpsimd):
+            engine.tensor_tensor(out=c_new[t][:], in0=c_new[t][:], in1=kept[t][:], op=ALU.add)
             nc.sync.dma_start(out=c_out[:, t, :], in_=c_new[t][:])
 
         def cell_mean(t):
@@ -393,7 +413,7 @@ def tile_layernormlstmcell_kernel(
             if 0 <= t < ROW_TILES:
                 stage_of(t, *more)
 
-        def round_of(i):
+        def round_start(i):
             on(gate_functions, i - 2)
             on(cell_products, i - 3)
             inverse_roots(i - 1, i - 4)
@@ -406,24 +426,83 @@ def tile_layernormlstmcell_kernel(
             on(cell_mean, i - 3)
             on(cell_tanh, i - 4)
             on(cell_squares, i - 3)
+
+        def round_end(i):
             on(shift_hh, i - 1)
             on(quantise_rows, i + 2)
             on(add_ih, i - 1, 0)
             on(sum_squares, i)
             on(add_ih, i - 1, 1)
             variances(i, i - 3)
-            on(flip_rows, i + 3)
             on(row_means, i + 1)
+            on(flip_rows, i + 3)
 
         with tc.manual_schedule():
-            spread(gain_rows[:, 0, :], gamma[0])
-            spread(gain_rows[:, 1, :], gamma[1])
-            for i in range(-3, 1):
-                round_of(i)
-            spread(shift_rows[:], beta_sum)
+            flip_rows(0)
+            quantise_rows(0)
+            spread(0, gamma[0])
+            flip_rows(1)
+            quantise_rows(1)
+            spread(1, gamma[1])
+            for s in range(2):
+                fold_passes(0, s)
+                fold_sum(0, s)
+                product(0, s)
+            flip_rows(2)
+            row_means(1)
+            quantise_rows(2)
+            spread(2, beta_sum)
+            sum_squares(0)
+            variances(0, -3)
+            round_start(1)
+            flip_rows(3)
+            round_end(1)
             for v in range(2):
-                nc.tensor.matmul(
-                    out=cell_vectors[:, v, :], lhsT=ones[:], rhs=cell_rows[:, v, :], start=True, stop=True
-                )
-            for i in range(1, ROW_TILES + 5):
-                round_of(i)
+                spread_bank(cell_vectors[:, v, :], 4 + v, slice(0, H))
+            for i in range(2, ROW_TILES):
+                round_start(i)
+                round_end(i)
+            last = ROW_TILES - 1
+            cell_products(last - 2)
+            inverse_roots(last, last - 3)
+            cell_sum(last - 2, nc.vector)
+            gate_functions(last - 1)
+            output_gate(last - 1)
+            shift_hh(last)
+            add_ih(last, 0)
+            add_ih(last, 1)
+            cell_mean(last - 2)
+            cell_squares(last - 2)
+            gate_functions(last)
+            output_gate(last)
+            cell_centre(last - 3)
+            cell_scale(last - 3)
+            cell_tanh(last - 3)
+            hidden_out(last - 4)
+            cell_products(last - 1, nc.vector)
+            cell_sum(last - 1, nc.vector)
+            variances(ROW_TILES, last - 2)
+            inverse_roots(ROW_TILES, last - 2)
+            cell_mean(last - 1)
+            cell_squares(last - 1)
+            cell_centre(last - 2)
+            cell_products(last, nc.vector)
+            cell_sum(last, nc.vector)
+            cell_scale(last - 2)
+            cell_tanh(last - 2)
+            cell_mean(last)
+            cell_squares(last)
+            hidden_out(last - 3)
+            variances(ROW_TILES + 1, last - 1)
+            inverse_roots(ROW_TILES + 1, last - 1)
+            cell_centre(last - 1)
+            cell_scale(last - 1)
+            cell_tanh(last - 1)
+            hidden_out(last - 2)
+            variances(ROW_TILES + 2, last)
+            inverse_roots(ROW_TILES + 2, last)
+            cell_centre(last)
+            cell_scale(last)
+            cell_tanh(last)
+            hidden_out(last - 1)
+            hidden_out(last)

@@ -72,39 +72,43 @@ def tile_layernormlstmcell_kernel(
         warm = const.tile([P, 1], F32)
         nc.scalar.activation(out=warm[:], in_=zero[:], func=ACT.Sigmoid)
 
-        vector_rows = const.tile([P, G], BF16)
-        nc.vector.memset(vector_rows[:].bitcast(I32), 0)
-        for row, vector in enumerate((gamma_ih, gamma_hh, beta_ih, beta_hh, gamma_c, beta_c)):
-            nc.scalar.dma_start(
-                out=vector_rows[row : row + 1, 0 : vector.shape[0]], in_=vector.unsqueeze(0)
-            )
+        vector_rows = [
+            const.tile([P, G], BF16, name="gamma_ih_row"),
+            const.tile([P, G], BF16, name="gamma_hh_row"),
+            const.tile([P, G], BF16, name="late_rows"),
+        ]
         w_scales = [
             const.tile([P, G], U8, name="w_ih_scales", align_bytes=64),
             const.tile([P, G], U8, name="w_hh_scales", align_bytes=64),
         ]
-        for plane in w_scales:
-            nc.vector.memset(plane[:].bitcast(I32), 0)
+        for zeroed in (vector_rows[0], w_scales[0], vector_rows[1], w_scales[1], vector_rows[2]):
+            nc.vector.memset(zeroed[:].bitcast(I32), 0)
         minus_half = const.tile([P, 3], F32)
         nc.vector.memset(minus_half[:], -0.5)
         ident = const.tile([P, P], F32)
         make_identity(nc, ident[:])
-        pick = const.tile([P, 6], BF16)
-        nc.scalar.copy(out=pick[:], in_=ident[:, 0:6])
-        nc.vector.tensor_tensor(out=pick[:, 2:3], in0=ident[:, 2:3], in1=ident[:, 3:4], op=ALU.add)
+        pick = const.tile([P, 4], BF16)
+        nc.scalar.copy(out=pick[:], in_=ident[:, 0:4])
+        nc.vector.tensor_tensor(out=pick[:, 1:2], in0=ident[:, 0:1], in1=ident[:, 1:2], op=ALU.add)
 
         x_sb = const.tile([P, ROW_TILES, K], BF16)
         h_sb = const.tile([P, ROW_TILES, K], BF16)
         c_sb = const.tile([P, ROW_TILES, H], BF16)
-        first = slice(0, FIRST_TILES)
-        nc.sync.dma_start(out=x_sb[:, first, :], in_=x_rows[:, first, :])
-        nc.sync.dma_start(out=h_sb[:, first, :], in_=h_rows[:, first, :])
         w_words = [
             const.tile([P, 4 * G], U8, name="w_ih_words", align_bytes=64),
             const.tile([P, 4 * G], U8, name="w_hh_words", align_bytes=64),
         ]
-        for s, (words, rows) in enumerate(
-            ((W_ih_words[0], W_ih_scales[0]), (W_hh_words[0], W_hh_scales[0]))
-        ):
+
+        def load_rows(tiles, *pairs):
+            for sbuf, dram in pairs:
+                nc.sync.dma_start(out=sbuf[:, tiles, :], in_=dram[:, tiles, :])
+
+        def load_vector(rows, row, vector):
+            nc.sync.dma_start(
+                out=rows[row : row + 1, 0 : vector.shape[0]], in_=vector.unsqueeze(0)
+            )
+
+        def load_weight(s, words, rows):
             for quad in range(4):
                 nc.sync.dma_start(
                     out=w_scales[s][32 * quad : 32 * quad + 4, :].bitcast(I32),
@@ -114,15 +118,20 @@ def tile_layernormlstmcell_kernel(
                 out=w_words[s][:].bitcast(I32),
                 in_=words.rearrange("p n t -> p (n t)").bitcast(I32),
             )
-        second = slice(FIRST_TILES, LOAD_TILES)
-        nc.sync.dma_start(out=x_sb[:, second, :], in_=x_rows[:, second, :])
-        nc.sync.dma_start(out=h_sb[:, second, :], in_=h_rows[:, second, :])
-        nc.sync.dma_start(out=c_sb[:, 0:LOAD_TILES, :], in_=c_rows[:, 0:LOAD_TILES, :])
+
+        load_rows(slice(0, FIRST_TILES), (x_sb, x_rows), (h_sb, h_rows))
+        load_vector(vector_rows[0], 0, gamma_ih)
+        load_weight(0, W_ih_words[0], W_ih_scales[0])
+        load_vector(vector_rows[1], 0, gamma_hh)
+        load_weight(1, W_hh_words[0], W_hh_scales[0])
+        load_vector(vector_rows[2], 0, beta_ih)
+        load_vector(vector_rows[2], 1, beta_hh)
+        load_rows(slice(FIRST_TILES, LOAD_TILES), (x_sb, x_rows), (h_sb, h_rows))
+        load_vector(vector_rows[2], 2, gamma_c)
+        load_vector(vector_rows[2], 3, beta_c)
+        load_rows(slice(0, LOAD_TILES), (c_sb, c_rows))
         for start in range(LOAD_TILES, ROW_TILES, LOAD_TILES):
-            chunk = slice(start, start + LOAD_TILES)
-            nc.sync.dma_start(out=x_sb[:, chunk, :], in_=x_rows[:, chunk, :])
-            nc.sync.dma_start(out=h_sb[:, chunk, :], in_=h_rows[:, chunk, :])
-            nc.sync.dma_start(out=c_sb[:, chunk, :], in_=c_rows[:, chunk, :])
+            load_rows(slice(start, start + LOAD_TILES), (x_sb, x_rows), (h_sb, h_rows), (c_sb, c_rows))
 
         gamma = [
             const.tile([P, G], BF16, name="gamma_ih_sb"),
@@ -133,20 +142,20 @@ def tile_layernormlstmcell_kernel(
         gamma_c_ps = cell_vectors[:, 0, :]
         beta_c_ps = cell_vectors[:, 1, :]
 
-        def spread_bank(acc, r, cols):
+        def spread_bank(acc, rows, r, cols):
             nc.tensor.matmul(
                 out=acc,
                 lhsT=pick[:, r : r + 1].to_broadcast([P, P]),
-                rhs=vector_rows[:, cols],
+                rhs=rows[:, cols],
                 start=True,
                 stop=True,
             )
 
-        def spread(r, out):
+        def spread(rows, r, out):
             for j in range(BANKS):
                 cols = slice(j * BANK, (j + 1) * BANK)
                 acc = psum_acc.tile([P, BANK], F32, name="acc")
-                spread_bank(acc[:], r, cols)
+                spread_bank(acc[:], rows, r, cols)
                 if j % 2 == 0:
                     nc.scalar.copy(out=out[:, cols], in_=acc[:])
                 else:
@@ -440,10 +449,10 @@ def tile_layernormlstmcell_kernel(
         with tc.manual_schedule():
             flip_rows(0)
             quantise_rows(0)
-            spread(0, gamma[0])
+            spread(vector_rows[0], 0, gamma[0])
             flip_rows(1)
             quantise_rows(1)
-            spread(1, gamma[1])
+            spread(vector_rows[1], 0, gamma[1])
             for s in range(2):
                 fold_passes(0, s)
                 fold_sum(0, s)
@@ -451,14 +460,14 @@ def tile_layernormlstmcell_kernel(
             flip_rows(2)
             row_means(1)
             quantise_rows(2)
-            spread(2, beta_sum)
+            spread(vector_rows[2], 1, beta_sum)
             sum_squares(0)
             variances(0, -3)
             round_start(1)
             flip_rows(3)
             round_end(1)
             for v in range(2):
-                spread_bank(cell_vectors[:, v, :], 4 + v, slice(0, H))
+                spread_bank(cell_vectors[:, v, :], vector_rows[2], 2 + v, slice(0, H))
             for i in range(2, ROW_TILES):
                 round_start(i)
                 round_end(i)
@@ -469,26 +478,26 @@ def tile_layernormlstmcell_kernel(
             gate_functions(last - 1)
             output_gate(last - 1)
             shift_hh(last)
+            cell_centre(last - 3)
             add_ih(last, 0)
+            cell_scale(last - 3)
             add_ih(last, 1)
             cell_mean(last - 2)
             cell_squares(last - 2)
-            gate_functions(last)
-            output_gate(last)
-            cell_centre(last - 3)
-            cell_scale(last - 3)
             cell_tanh(last - 3)
             hidden_out(last - 4)
+            gate_functions(last)
+            output_gate(last)
             cell_products(last - 1, nc.vector)
-            cell_sum(last - 1, nc.vector)
             variances(ROW_TILES, last - 2)
             inverse_roots(ROW_TILES, last - 2)
+            cell_sum(last - 1, nc.vector)
+            cell_centre(last - 2)
             cell_mean(last - 1)
             cell_squares(last - 1)
-            cell_centre(last - 2)
             cell_products(last, nc.vector)
-            cell_sum(last, nc.vector)
             cell_scale(last - 2)
+            cell_sum(last, nc.vector)
             cell_tanh(last - 2)
             cell_mean(last)
             cell_squares(last)
@@ -496,13 +505,13 @@ def tile_layernormlstmcell_kernel(
             variances(ROW_TILES + 1, last - 1)
             inverse_roots(ROW_TILES + 1, last - 1)
             cell_centre(last - 1)
+            hidden_out(last - 2)
             cell_scale(last - 1)
             cell_tanh(last - 1)
-            hidden_out(last - 2)
             variances(ROW_TILES + 2, last)
             inverse_roots(ROW_TILES + 2, last)
             cell_centre(last)
             cell_scale(last)
-            cell_tanh(last)
             hidden_out(last - 1)
+            cell_tanh(last)
             hidden_out(last)

@@ -56,10 +56,8 @@ def tile_layernormlstmcell_kernel(
         wide_ih = ctx.enter_context(tc.tile_pool(name="wide_ih", bufs=4))
         wide_hh = ctx.enter_context(tc.tile_pool(name="wide_hh", bufs=2))
         narrow = ctx.enter_context(tc.tile_pool(name="narrow", bufs=4))
-        psum_flip = ctx.enter_context(tc.psum_pool(name="psum_flip", bufs=1))
-        psum_fold = ctx.enter_context(tc.psum_pool(name="psum_fold", bufs=1))
         psum_cell = ctx.enter_context(tc.psum_pool(name="psum_cell", bufs=1))
-        psum_acc = ctx.enter_context(tc.psum_pool(name="psum_acc", bufs=5))
+        psum_acc = ctx.enter_context(tc.psum_pool(name="psum_acc", bufs=7))
 
         x_rows = x.rearrange("(p t) k -> p t k", t=ROW_TILES)
         h_rows = h_prev.rearrange("(p t) k -> p t k", t=ROW_TILES)
@@ -179,7 +177,7 @@ def tile_layernormlstmcell_kernel(
         normed = {}
 
         def flip_rows(t):
-            flipped = psum_flip.tile([P, 2, 2, P], F32)
+            flipped = psum_acc.tile([P, 2, 2, P], F32, name="acc")
             for s, rows in enumerate((x_sb, h_sb)):
                 words = rows[:, t, :].bitcast(F32)
                 for u in range(2):
@@ -214,7 +212,7 @@ def tile_layernormlstmcell_kernel(
 
         def fold_passes(t, s):
             if s == 0:
-                fold[t] = psum_fold.tile([P, 2, FOLD], F32, name="fold")
+                fold[t] = psum_acc.tile([P, 2, FOLD], F32, name="acc")
             for j in range(G // FOLD):
                 mx_pass(fold[t][:, s, :], t, s, j * FOLD, FOLD, j == 0, j == G // FOLD - 1)
 

@@ -56,8 +56,7 @@ def tile_layernormlstmcell_kernel(
         wide_ih = ctx.enter_context(tc.tile_pool(name="wide_ih", bufs=4))
         wide_hh = ctx.enter_context(tc.tile_pool(name="wide_hh", bufs=2))
         narrow = ctx.enter_context(tc.tile_pool(name="narrow", bufs=4))
-        psum_cell = ctx.enter_context(tc.psum_pool(name="psum_cell", bufs=1))
-        psum_acc = ctx.enter_context(tc.psum_pool(name="psum_acc", bufs=7))
+        psum_acc = ctx.enter_context(tc.psum_pool(name="psum_acc", bufs=8))
 
         x_rows = x.rearrange("(p t) k -> p t k", t=ROW_TILES)
         h_rows = h_prev.rearrange("(p t) k -> p t k", t=ROW_TILES)
@@ -136,9 +135,7 @@ def tile_layernormlstmcell_kernel(
             const.tile([P, G], BF16, name="gamma_hh_sb"),
         ]
         beta_sum = const.tile([P, G], F32)
-        cell_vectors = psum_cell.tile([P, 2, H], BF16)
-        gamma_c_ps = cell_vectors[:, 0, :]
-        beta_c_ps = cell_vectors[:, 1, :]
+        cell_cols = const.tile([P, H // P, 2], F32)
 
         def spread_bank(acc, rows, r, cols):
             nc.tensor.matmul(
@@ -160,6 +157,9 @@ def tile_layernormlstmcell_kernel(
                     nc.vector.tensor_copy(out=out[:, cols], in_=acc[:])
 
         grouped = {}
+        turned = {}
+        tanh_t = {}
+        back = {}
         fold = {}
         rows_mx = {}
         neg_mean = {}
@@ -183,7 +183,7 @@ def tile_layernormlstmcell_kernel(
                 for u in range(2):
                     nc.tensor.transpose(flipped[:, s, u, :], words[:, u : K // 2 : 2], ident[:])
             grouped[t] = stage.tile([P, 2, P, 4], BF16, name="grouped", align_bytes=64)
-            nc.scalar.copy(
+            nc.vector.tensor_copy(
                 out=grouped[t][:].bitcast(F32), in_=flipped[:].rearrange("p s u r -> p s r u")
             )
 
@@ -387,33 +387,38 @@ def tile_layernormlstmcell_kernel(
                 accum_out=sq_sum_c[t][:],
             )
 
-        def cell_centre(t):
+        def cell_normalise(t):
+            shift = stats.tile([P, 1], F32, name="shift_c")
+            nc.scalar.activation(out=shift[:], in_=neg_mean_c[t][:], func=ACT.Copy, scale=rstd_c[t])
             normed[t] = narrow.tile([P, H], F32, name="normed")
-            nc.vector.scalar_tensor_tensor(
-                out=normed[t][:],
-                in0=c_new[t][:],
-                scalar=neg_mean_c[t][:],
-                in1=gamma_c_ps,
-                op0=ALU.add,
-                op1=ALU.mult,
+            nc.scalar.activation(
+                out=normed[t][:], in_=c_new[t][:], func=ACT.Identity, scale=rstd_c[t], bias=shift[:]
             )
 
-        def cell_scale(t):
-            nc.vector.scalar_tensor_tensor(
-                out=normed[t][:],
-                in0=normed[t][:],
-                scalar=rstd_c[t],
-                in1=beta_c_ps,
-                op0=ALU.mult,
-                op1=ALU.add,
-            )
+        def cell_turn(t):
+            turned[t] = psum_acc.tile([P, H // P, P], F32, name="acc")
+            for b in range(H // P):
+                nc.tensor.transpose(turned[t][:, b, :], normed[t][:, b * P : (b + 1) * P], ident[:])
 
         def cell_tanh(t):
-            nc.scalar.activation(out=normed[t][:], in_=normed[t][:], func=ACT.Tanh)
+            tanh_t[t] = narrow.tile([P, H // P, P], F32, name="tanh_t")
+            for b in range(H // P):
+                nc.scalar.activation(
+                    out=tanh_t[t][:, b, :],
+                    in_=turned[t][:, b, :],
+                    func=ACT.Tanh,
+                    scale=cell_cols[:, b, 0:1],
+                    bias=cell_cols[:, b, 1:2],
+                )
+
+        def cell_turn_back(t):
+            back[t] = psum_acc.tile([P, H], F32, name="acc")
+            for b in range(H // P):
+                nc.tensor.transpose(back[t][:, b * P : (b + 1) * P], tanh_t[t][:, b, :], ident[:])
 
         def hidden_out(t):
             h_new = narrow.tile([P, H], F32)
-            nc.vector.tensor_tensor(out=h_new[:], in0=o_gate[t][:], in1=normed[t][:], op=ALU.mult)
+            nc.vector.tensor_tensor(out=h_new[:], in0=o_gate[t][:], in1=back[t][:], op=ALU.mult)
             nc.sync.dma_start(out=h_out[:, t, :], in_=h_new[:])
 
         def on(stage_of, t, *more):
@@ -425,24 +430,25 @@ def tile_layernormlstmcell_kernel(
             on(cell_products, i - 3)
             inverse_roots(i - 1, i - 4)
             on(cell_sum, i - 3)
-            on(cell_centre, i - 4)
-            on(products, i)
-            on(cell_scale, i - 4)
+            on(cell_normalise, i - 4)
             on(hidden_out, i - 5)
+            on(products, i)
+            on(cell_turn, i - 4)
             on(output_gate, i - 2)
             on(cell_mean, i - 3)
-            on(cell_tanh, i - 4)
             on(cell_squares, i - 3)
+            on(cell_tanh, i - 4)
 
         def round_end(i):
             on(shift_hh, i - 1)
             on(quantise_rows, i + 2)
             on(add_ih, i - 1, 0)
             on(sum_squares, i)
-            on(add_ih, i - 1, 1)
             variances(i, i - 3)
+            on(add_ih, i - 1, 1)
             on(row_means, i + 1)
             on(flip_rows, i + 3)
+            on(cell_turn_back, i - 4)
 
         with tc.manual_schedule():
             flip_rows(0)
@@ -464,8 +470,16 @@ def tile_layernormlstmcell_kernel(
             round_start(1)
             flip_rows(3)
             round_end(1)
-            for v in range(2):
-                spread_bank(cell_vectors[:, v, :], vector_rows[2], 2 + v, slice(0, H))
+            cols_ps = psum_acc.tile([P, H // P, 2], F32, name="acc")
+            for b in range(H // P):
+                nc.tensor.matmul(
+                    out=cols_ps[:, b, :],
+                    lhsT=vector_rows[2][:, b * P : (b + 1) * P],
+                    rhs=pick[:, 2:4],
+                    start=True,
+                    stop=True,
+                )
+            nc.scalar.copy(out=cell_cols[:], in_=cols_ps[:])
             for i in range(2, ROW_TILES):
                 round_start(i)
                 round_end(i)
@@ -475,41 +489,45 @@ def tile_layernormlstmcell_kernel(
             cell_sum(last - 2, nc.vector)
             gate_functions(last - 1)
             output_gate(last - 1)
+            cell_normalise(last - 3)
+            cell_turn(last - 3)
             shift_hh(last)
-            cell_centre(last - 3)
+            cell_products(last - 1, nc.vector)
             add_ih(last, 0)
-            cell_scale(last - 3)
+            cell_sum(last - 1, nc.vector)
             add_ih(last, 1)
             cell_mean(last - 2)
             cell_squares(last - 2)
             cell_tanh(last - 3)
+            cell_turn_back(last - 3)
             hidden_out(last - 4)
             gate_functions(last)
             output_gate(last)
-            cell_products(last - 1, nc.vector)
-            variances(ROW_TILES, last - 2)
-            inverse_roots(ROW_TILES, last - 2)
-            cell_sum(last - 1, nc.vector)
-            cell_centre(last - 2)
             cell_mean(last - 1)
             cell_squares(last - 1)
+            variances(ROW_TILES, last - 2)
+            inverse_roots(ROW_TILES, last - 2)
             cell_products(last, nc.vector)
-            cell_scale(last - 2)
             cell_sum(last, nc.vector)
-            cell_tanh(last - 2)
+            cell_normalise(last - 2)
+            cell_turn(last - 2)
+            variances(ROW_TILES + 1, last - 1)
+            inverse_roots(ROW_TILES + 1, last - 1)
             cell_mean(last)
             cell_squares(last)
             hidden_out(last - 3)
-            variances(ROW_TILES + 1, last - 1)
-            inverse_roots(ROW_TILES + 1, last - 1)
-            cell_centre(last - 1)
-            hidden_out(last - 2)
-            cell_scale(last - 1)
-            cell_tanh(last - 1)
+            cell_tanh(last - 2)
+            cell_turn_back(last - 2)
             variances(ROW_TILES + 2, last)
             inverse_roots(ROW_TILES + 2, last)
-            cell_centre(last)
-            cell_scale(last)
-            hidden_out(last - 1)
+            cell_normalise(last - 1)
+            cell_turn(last - 1)
+            cell_normalise(last)
+            cell_turn(last)
+            hidden_out(last - 2)
+            cell_tanh(last - 1)
+            cell_turn_back(last - 1)
             cell_tanh(last)
+            cell_turn_back(last)
+            hidden_out(last - 1)
             hidden_out(last)

@@ -444,8 +444,8 @@ def tile_layernormlstmcell_kernel(
             on(quantise_rows, i + 2)
             on(add_ih, i - 1, 0)
             on(sum_squares, i)
-            variances(i, i - 3)
             on(add_ih, i - 1, 1)
+            variances(i, i - 3)
             on(row_means, i + 1)
             on(flip_rows, i + 3)
             on(cell_turn_back, i - 4)
@@ -508,6 +508,7 @@ def tile_layernormlstmcell_kernel(
             variances(ROW_TILES, last - 2)
             inverse_roots(ROW_TILES, last - 2)
             cell_products(last, nc.vector)
+            hidden_out(last - 3)
             cell_sum(last, nc.vector)
             cell_normalise(last - 2)
             cell_turn(last - 2)
@@ -515,7 +516,6 @@ def tile_layernormlstmcell_kernel(
             inverse_roots(ROW_TILES + 1, last - 1)
             cell_mean(last)
             cell_squares(last)
-            hidden_out(last - 3)
             cell_tanh(last - 2)
             cell_turn_back(last - 2)
             variances(ROW_TILES + 2, last)

@@ -136,6 +136,7 @@ def tile_layernormlstmcell_kernel(
         ]
         beta_sum = const.tile([P, G], F32)
         cell_cols = const.tile([P, H // P, 2], F32)
+        cell_spread = const.tile([P, 2, H], BF16)
 
         def spread_bank(acc, rows, r, cols):
             nc.tensor.matmul(
@@ -421,6 +422,35 @@ def tile_layernormlstmcell_kernel(
             nc.vector.tensor_tensor(out=h_new[:], in0=o_gate[t][:], in1=back[t][:], op=ALU.mult)
             nc.sync.dma_start(out=h_out[:, t, :], in_=h_new[:])
 
+        def direct_centre(t):
+            normed[t] = narrow.tile([P, H], F32, name="normed")
+            nc.vector.scalar_tensor_tensor(
+                out=normed[t][:],
+                in0=c_new[t][:],
+                scalar=neg_mean_c[t][:],
+                in1=cell_spread[:, 0, :],
+                op0=ALU.add,
+                op1=ALU.mult,
+            )
+
+        def direct_scale(t):
+            nc.vector.scalar_tensor_tensor(
+                out=normed[t][:],
+                in0=normed[t][:],
+                scalar=rstd_c[t],
+                in1=cell_spread[:, 1, :],
+                op0=ALU.mult,
+                op1=ALU.add,
+            )
+
+        def direct_tanh(t):
+            nc.scalar.activation(out=normed[t][:], in_=normed[t][:], func=ACT.Tanh)
+
+        def direct_hidden(t):
+            h_new = narrow.tile([P, H], F32, name="h_new")
+            nc.vector.tensor_tensor(out=h_new[:], in0=o_gate[t][:], in1=normed[t][:], op=ALU.mult)
+            nc.sync.dma_start(out=h_out[:, t, :], in_=h_new[:])
+
         def on(stage_of, t, *more):
             if 0 <= t < ROW_TILES:
                 stage_of(t, *more)
@@ -480,6 +510,10 @@ def tile_layernormlstmcell_kernel(
                     stop=True,
                 )
             nc.scalar.copy(out=cell_cols[:], in_=cols_ps[:])
+            for v in range(2):
+                acc = psum_acc.tile([P, BANK], F32, name="acc")
+                spread_bank(acc[:], vector_rows[2], 2 + v, slice(0, H))
+                nc.scalar.copy(out=cell_spread[:, v, :], in_=acc[:])
             for i in range(2, ROW_TILES):
                 round_start(i)
                 round_end(i)
@@ -512,22 +546,20 @@ def tile_layernormlstmcell_kernel(
             cell_sum(last, nc.vector)
             cell_normalise(last - 2)
             cell_turn(last - 2)
+            direct_centre(last - 1)
             variances(ROW_TILES + 1, last - 1)
             inverse_roots(ROW_TILES + 1, last - 1)
             cell_mean(last)
             cell_squares(last)
             cell_tanh(last - 2)
             cell_turn_back(last - 2)
+            direct_centre(last)
+            direct_scale(last - 1)
             variances(ROW_TILES + 2, last)
             inverse_roots(ROW_TILES + 2, last)
-            cell_normalise(last - 1)
-            cell_turn(last - 1)
-            cell_normalise(last)
-            cell_turn(last)
+            direct_tanh(last - 1)
+            direct_scale(last)
+            direct_tanh(last)
+            direct_hidden(last - 1)
             hidden_out(last - 2)
-            cell_tanh(last - 1)
-            cell_turn_back(last - 1)
-            cell_tanh(last)
-            cell_turn_back(last)
-            hidden_out(last - 1)
-            hidden_out(last)
+            direct_hidden(last)

@@ -461,9 +461,10 @@ def tile_layernormlstmcell_kernel(
             inverse_roots(i - 1, i - 4)
             on(cell_sum, i - 3)
             on(cell_normalise, i - 4)
-            on(hidden_out, i - 5)
             on(products, i)
+            on(cell_turn_back, i - 5)
             on(cell_turn, i - 4)
+            on(hidden_out, i - 5)
             on(output_gate, i - 2)
             on(cell_mean, i - 3)
             on(cell_squares, i - 3)
@@ -478,7 +479,6 @@ def tile_layernormlstmcell_kernel(
             variances(i, i - 3)
             on(row_means, i + 1)
             on(flip_rows, i + 3)
-            on(cell_turn_back, i - 4)
 
         with tc.manual_schedule():
             flip_rows(0)
@@ -518,6 +518,7 @@ def tile_layernormlstmcell_kernel(
                 round_start(i)
                 round_end(i)
             last = ROW_TILES - 1
+            cell_turn_back(last - 4)
             cell_products(last - 2)
             inverse_roots(last, last - 3)
             cell_sum(last - 2, nc.vector)

@@ -158,6 +158,7 @@ def tile_layernormlstmcell_kernel(
                     nc.vector.tensor_copy(out=out[:, cols], in_=acc[:])
 
         grouped = {}
+        shift_c = {}
         turned = {}
         tanh_t = {}
         back = {}
@@ -338,12 +339,19 @@ def tile_layernormlstmcell_kernel(
                 op1=ALU.add,
             )
 
-        def gate_functions(t):
+        def gate_sigmoids(t):
             gates = scaled[t][0]
             nc.scalar.activation(out=gates[:, 0 : 2 * H], in_=gates[:, 0 : 2 * H], func=ACT.Sigmoid)
+
+        def gate_tanh(t):
+            gates = scaled[t][0]
             nc.scalar.activation(
                 out=gates[:, 2 * H : 3 * H], in_=gates[:, 2 * H : 3 * H], func=ACT.Tanh
             )
+
+        def gate_functions(t):
+            gate_sigmoids(t)
+            gate_tanh(t)
 
         def output_gate(t):
             o_gate[t] = narrow.tile([P, H], F32, name="o_gate")
@@ -388,13 +396,19 @@ def tile_layernormlstmcell_kernel(
                 accum_out=sq_sum_c[t][:],
             )
 
-        def cell_normalise(t):
-            shift = stats.tile([P, 1], F32, name="shift_c")
-            nc.scalar.activation(out=shift[:], in_=neg_mean_c[t][:], func=ACT.Copy, scale=rstd_c[t])
+        def cell_shift(t):
+            shift_c[t] = stats.tile([P, 1], F32, name="shift_c")
+            nc.scalar.activation(out=shift_c[t][:], in_=neg_mean_c[t][:], func=ACT.Copy, scale=rstd_c[t])
+
+        def cell_scale(t):
             normed[t] = narrow.tile([P, H], F32, name="normed")
             nc.scalar.activation(
-                out=normed[t][:], in_=c_new[t][:], func=ACT.Identity, scale=rstd_c[t], bias=shift[:]
+                out=normed[t][:], in_=c_new[t][:], func=ACT.Identity, scale=rstd_c[t], bias=shift_c[t][:]
             )
+
+        def cell_normalise(t):
+            cell_shift(t)
+            cell_scale(t)
 
         def cell_turn(t):
             turned[t] = psum_acc.tile([P, H // P, P], F32, name="acc")
@@ -456,17 +470,19 @@ def tile_layernormlstmcell_kernel(
                 stage_of(t, *more)
 
         def round_start(i):
-            on(gate_functions, i - 2)
+            on(gate_sigmoids, i - 2)
             on(cell_products, i - 3)
             inverse_roots(i - 1, i - 4)
             on(cell_sum, i - 3)
-            on(cell_normalise, i - 4)
+            on(cell_shift, i - 4)
+            on(gate_tanh, i - 2)
+            on(cell_scale, i - 4)
             on(products, i)
             on(cell_turn_back, i - 5)
             on(cell_turn, i - 4)
             on(hidden_out, i - 5)
-            on(output_gate, i - 2)
             on(cell_mean, i - 3)
+            on(output_gate, i - 2)
             on(cell_squares, i - 3)
             on(cell_tanh, i - 4)
 

@@ -25,6 +25,9 @@ BANKS = G // BANK
 FOLD = 128
 LOAD_TILES = 4
 FIRST_TILES = 2
+ROOT_G = G**0.5
+ROOT_H = H**0.5
+SUM_RING = 4
 
 FLOPS = 2 * 2 * B * K * G
 
@@ -82,6 +85,19 @@ def tile_layernormlstmcell_kernel(
             nc.vector.memset(zeroed[:].bitcast(I32), 0)
         minus_half = const.tile([P, 3], F32)
         nc.vector.memset(minus_half[:], -0.5)
+        sums = [const.tile([P, 3, BANKS + 1], F32, name="sums%d" % r) for r in range(SUM_RING)]
+        for ring_tile in sums:
+            nc.vector.memset(ring_tile[:], 0.0)
+        for ring_tile in sums:
+            for rows, length in ((slice(0, 2), G), (slice(2, 3), H)):
+                nc.vector.tensor_scalar(
+                    out=ring_tile[:, rows, BANKS : BANKS + 1],
+                    in0=ring_tile[:, rows, BANKS : BANKS + 1],
+                    scalar1=1.0,
+                    scalar2=EPS * length,
+                    op0=ALU.mult,
+                    op1=ALU.add,
+                )
         ident = const.tile([P, P], F32)
         make_identity(nc, ident[:])
         pick = const.tile([P, 4], BF16)
@@ -136,7 +152,7 @@ def tile_layernormlstmcell_kernel(
         ]
         beta_sum = const.tile([P, G], F32)
         cell_cols = const.tile([P, H // P, 2], F32)
-        cell_spread = const.tile([P, 2, H], BF16)
+        cell_spread = const.tile([P, 2, H], F32)
 
         def spread_bank(acc, rows, r, cols):
             nc.tensor.matmul(
@@ -147,15 +163,17 @@ def tile_layernormlstmcell_kernel(
                 stop=True,
             )
 
-        def spread(rows, r, out):
+        def spread(rows, r, out, factor):
             for j in range(BANKS):
                 cols = slice(j * BANK, (j + 1) * BANK)
                 acc = psum_acc.tile([P, BANK], F32, name="acc")
                 spread_bank(acc[:], rows, r, cols)
                 if j % 2 == 0:
-                    nc.scalar.copy(out=out[:, cols], in_=acc[:])
+                    nc.scalar.activation(out=out[:, cols], in_=acc[:], func=ACT.Copy, scale=factor)
                 else:
-                    nc.vector.tensor_copy(out=out[:, cols], in_=acc[:])
+                    nc.vector.tensor_scalar(
+                        out=out[:, cols], in0=acc[:], scalar1=factor, scalar2=None, op0=ALU.mult
+                    )
 
         grouped = {}
         shift_c = {}
@@ -165,8 +183,6 @@ def tile_layernormlstmcell_kernel(
         fold = {}
         rows_mx = {}
         neg_mean = {}
-        sq_part = {}
-        sq_sum = {}
         var = {}
         kept = {}
         scaled = {}
@@ -174,7 +190,6 @@ def tile_layernormlstmcell_kernel(
         o_gate = {}
         c_new = {}
         neg_mean_c = {}
-        sq_sum_c = {}
         rstd_c = {}
         normed = {}
 
@@ -185,7 +200,7 @@ def tile_layernormlstmcell_kernel(
                 for u in range(2):
                     nc.tensor.transpose(flipped[:, s, u, :], words[:, u : K // 2 : 2], ident[:])
             grouped[t] = stage.tile([P, 2, P, 4], BF16, name="grouped", align_bytes=64)
-            nc.vector.tensor_copy(
+            nc.scalar.copy(
                 out=grouped[t][:].bitcast(F32), in_=flipped[:].rearrange("p s u r -> p s r u")
             )
 
@@ -238,7 +253,6 @@ def tile_layernormlstmcell_kernel(
 
         def product(t, s):
             if s == 0:
-                sq_part[t] = stats.tile([P, 2, BANKS], F32, name="sq_part")
                 scaled[t] = (
                     wide_ih.tile([P, G], F32, name="scaled_ih"),
                     wide_hh.tile([P, G], F32, name="scaled_hh"),
@@ -261,16 +275,12 @@ def tile_layernormlstmcell_kernel(
                     in_=acc[:],
                     func=ACT.Square,
                     bias=neg_mean[t][:, s : s + 1],
-                    accum_out=sq_part[t][:, s, j : j + 1],
+                    accum_out=sums[t % SUM_RING][:, s, j : j + 1],
                 )
 
         def products(t):
             product(t, 0)
             product(t, 1)
-
-        def sum_squares(t):
-            sq_sum[t] = stats.tile([P, 2], F32, name="sq_sum")
-            nc.vector.tensor_reduce(out=sq_sum[t][:], in_=sq_part[t][:], axis=AX.X, op=ALU.add)
 
         def live_columns(gate_tile, cell_tile):
             first_col = 0 if 0 <= gate_tile < ROW_TILES else 2
@@ -281,25 +291,14 @@ def tile_layernormlstmcell_kernel(
             first_col, end_col = live_columns(gate_tile, cell_tile)
             if first_col == end_col:
                 return
+            live = slice(first_col, end_col)
             var[gate_tile] = stats.tile([P, 3], F32, name="var")
-            if first_col == 0:
-                nc.vector.tensor_scalar(
-                    out=var[gate_tile][:, 0:2],
-                    in0=sq_sum[gate_tile][:],
-                    scalar1=1.0 / G,
-                    scalar2=EPS,
-                    op0=ALU.mult,
-                    op1=ALU.add,
-                )
-            if end_col == 3:
-                nc.vector.tensor_scalar(
-                    out=var[gate_tile][:, 2:3],
-                    in0=sq_sum_c[cell_tile][:],
-                    scalar1=1.0 / H,
-                    scalar2=EPS,
-                    op0=ALU.mult,
-                    op1=ALU.add,
-                )
+            nc.vector.tensor_reduce(
+                out=var[gate_tile][:, live],
+                in_=sums[gate_tile % SUM_RING][:, live, :],
+                axis=AX.X,
+                op=ALU.add,
+            )
 
         def inverse_roots(gate_tile, cell_tile):
             first_col, end_col = live_columns(gate_tile, cell_tile)
@@ -341,12 +340,14 @@ def tile_layernormlstmcell_kernel(
 
         def gate_sigmoids(t):
             gates = scaled[t][0]
-            nc.scalar.activation(out=gates[:, 0 : 2 * H], in_=gates[:, 0 : 2 * H], func=ACT.Sigmoid)
+            nc.scalar.activation(
+                out=gates[:, 0 : 2 * H], in_=gates[:, 0 : 2 * H], func=ACT.Sigmoid, scale=ROOT_G
+            )
 
         def gate_tanh(t):
             gates = scaled[t][0]
             nc.scalar.activation(
-                out=gates[:, 2 * H : 3 * H], in_=gates[:, 2 * H : 3 * H], func=ACT.Tanh
+                out=gates[:, 2 * H : 3 * H], in_=gates[:, 2 * H : 3 * H], func=ACT.Tanh, scale=ROOT_G
             )
 
         def gate_functions(t):
@@ -356,7 +357,7 @@ def tile_layernormlstmcell_kernel(
         def output_gate(t):
             o_gate[t] = narrow.tile([P, H], F32, name="o_gate")
             nc.scalar.activation(
-                out=o_gate[t][:], in_=scaled[t][0][:, 3 * H : 4 * H], func=ACT.Sigmoid
+                out=o_gate[t][:], in_=scaled[t][0][:, 3 * H : 4 * H], func=ACT.Sigmoid, scale=ROOT_G
             )
 
         def cell_products(t, engine=nc.gpsimd):
@@ -386,14 +387,13 @@ def tile_layernormlstmcell_kernel(
             )
 
         def cell_squares(t):
-            sq_sum_c[t] = stats.tile([P, 1], F32, name="sq_sum_c")
             scrap = stage.tile([P, BANK], BF16, name="scrap")
             nc.scalar.activation(
                 out=scrap[:],
                 in_=c_new[t][:],
                 func=ACT.Square,
                 bias=neg_mean_c[t][:],
-                accum_out=sq_sum_c[t][:],
+                accum_out=sums[(t + 3) % SUM_RING][:, 2, 0:1],
             )
 
         def cell_shift(t):
@@ -409,6 +409,17 @@ def tile_layernormlstmcell_kernel(
         def cell_normalise(t):
             cell_shift(t)
             cell_scale(t)
+
+        def cell_normalise_beside(t):
+            normed[t] = narrow.tile([P, H], F32, name="normed")
+            nc.gpsimd.tensor_scalar(
+                out=normed[t][:],
+                in0=c_new[t][:],
+                scalar1=neg_mean_c[t][:],
+                scalar2=rstd_c[t],
+                op0=ALU.add,
+                op1=ALU.mult,
+            )
 
         def cell_turn(t):
             turned[t] = psum_acc.tile([P, H // P, P], F32, name="acc")
@@ -458,7 +469,7 @@ def tile_layernormlstmcell_kernel(
             )
 
         def direct_tanh(t):
-            nc.scalar.activation(out=normed[t][:], in_=normed[t][:], func=ACT.Tanh)
+            nc.scalar.activation(out=normed[t][:], in_=normed[t][:], func=ACT.Tanh, scale=ROOT_H)
 
         def direct_hidden(t):
             h_new = narrow.tile([P, H], F32, name="h_new")
@@ -474,9 +485,8 @@ def tile_layernormlstmcell_kernel(
             on(cell_products, i - 3)
             inverse_roots(i - 1, i - 4)
             on(cell_sum, i - 3)
-            on(cell_shift, i - 4)
+            on(cell_normalise_beside, i - 4)
             on(gate_tanh, i - 2)
-            on(cell_scale, i - 4)
             on(products, i)
             on(cell_turn_back, i - 5)
             on(cell_turn, i - 4)
@@ -490,7 +500,6 @@ def tile_layernormlstmcell_kernel(
             on(shift_hh, i - 1)
             on(quantise_rows, i + 2)
             on(add_ih, i - 1, 0)
-            on(sum_squares, i)
             on(add_ih, i - 1, 1)
             variances(i, i - 3)
             on(row_means, i + 1)
@@ -499,10 +508,10 @@ def tile_layernormlstmcell_kernel(
         with tc.manual_schedule():
             flip_rows(0)
             quantise_rows(0)
-            spread(vector_rows[0], 0, gamma[0])
+            spread(vector_rows[0], 0, gamma[0], 1.0)
             flip_rows(1)
             quantise_rows(1)
-            spread(vector_rows[1], 0, gamma[1])
+            spread(vector_rows[1], 0, gamma[1], 1.0)
             for s in range(2):
                 fold_passes(0, s)
                 fold_sum(0, s)
@@ -510,8 +519,7 @@ def tile_layernormlstmcell_kernel(
             flip_rows(2)
             row_means(1)
             quantise_rows(2)
-            spread(vector_rows[2], 1, beta_sum)
-            sum_squares(0)
+            spread(vector_rows[2], 1, beta_sum, 1.0 / ROOT_G)
             variances(0, -3)
             round_start(1)
             flip_rows(3)
@@ -525,11 +533,14 @@ def tile_layernormlstmcell_kernel(
                     start=True,
                     stop=True,
                 )
-            nc.scalar.copy(out=cell_cols[:], in_=cols_ps[:])
-            for v in range(2):
+            nc.scalar.activation(
+                out=cell_cols[:, :, 0:1], in_=cols_ps[:, :, 0:1], func=ACT.Copy, scale=ROOT_H
+            )
+            nc.scalar.copy(out=cell_cols[:, :, 1:2], in_=cols_ps[:, :, 1:2])
+            for v, factor in enumerate((1.0, 1.0 / ROOT_H)):
                 acc = psum_acc.tile([P, BANK], F32, name="acc")
                 spread_bank(acc[:], vector_rows[2], 2 + v, slice(0, H))
-                nc.scalar.copy(out=cell_spread[:, v, :], in_=acc[:])
+                nc.scalar.activation(out=cell_spread[:, v, :], in_=acc[:], func=ACT.Copy, scale=factor)
             for i in range(2, ROW_TILES):
                 round_start(i)
                 round_end(i)

@@ -26,6 +26,7 @@ FOLD = 128
 LOAD_TILES = 4
 FIRST_TILES = 2
 ROOT_G = G**0.5
+BETA_BANKS = 2
 ROOT_H = H**0.5
 SUM_RING = 4
 
@@ -59,7 +60,8 @@ def tile_layernormlstmcell_kernel(
         wide_ih = ctx.enter_context(tc.tile_pool(name="wide_ih", bufs=4))
         wide_hh = ctx.enter_context(tc.tile_pool(name="wide_hh", bufs=2))
         narrow = ctx.enter_context(tc.tile_pool(name="narrow", bufs=4))
-        psum_acc = ctx.enter_context(tc.psum_pool(name="psum_acc", bufs=8))
+        psum_acc = ctx.enter_context(tc.psum_pool(name="psum_acc", bufs=8 - BETA_BANKS))
+        psum_keep = ctx.enter_context(tc.psum_pool(name="psum_keep", bufs=1))
 
         x_rows = x.rearrange("(p t) k -> p t k", t=ROW_TILES)
         h_rows = h_prev.rearrange("(p t) k -> p t k", t=ROW_TILES)
@@ -147,10 +149,11 @@ def tile_layernormlstmcell_kernel(
             load_rows(slice(start, start + LOAD_TILES), (x_sb, x_rows), (h_sb, h_rows), (c_sb, c_rows))
 
         gamma = [
-            const.tile([P, G], BF16, name="gamma_ih_sb"),
-            const.tile([P, G], BF16, name="gamma_hh_sb"),
+            const.tile([P, G], F32, name="gamma_ih_sb"),
+            const.tile([P, G], F32, name="gamma_hh_sb"),
         ]
         beta_sum = const.tile([P, G], F32)
+        beta_kept = [psum_keep.tile([P, BANK], F32, name="beta_kept%d" % j) for j in range(BETA_BANKS)]
         cell_cols = const.tile([P, H // P, 2], F32)
         cell_spread = const.tile([P, 2, H], F32)
 
@@ -163,8 +166,8 @@ def tile_layernormlstmcell_kernel(
                 stop=True,
             )
 
-        def spread(rows, r, out, factor):
-            for j in range(BANKS):
+        def spread(rows, r, out, factor, first_bank=0):
+            for j in range(first_bank, BANKS):
                 cols = slice(j * BANK, (j + 1) * BANK)
                 acc = psum_acc.tile([P, BANK], F32, name="acc")
                 spread_bank(acc[:], rows, r, cols)
@@ -317,14 +320,17 @@ def tile_layernormlstmcell_kernel(
 
         def shift_hh(t):
             scaled_hh = scaled[t][1]
-            nc.vector.scalar_tensor_tensor(
-                out=scaled_hh[:],
-                in0=scaled_hh[:],
-                scalar=rstd[t][:, 1:2],
-                in1=beta_sum[:],
-                op0=ALU.mult,
-                op1=ALU.add,
-            )
+            rest = slice(BETA_BANKS * BANK, G)
+            pieces = [(slice(j * BANK, (j + 1) * BANK), beta_kept[j][:]) for j in range(BETA_BANKS)]
+            for cols, beta_cols in pieces + [(rest, beta_sum[:, rest])]:
+                nc.vector.scalar_tensor_tensor(
+                    out=scaled_hh[:, cols],
+                    in0=scaled_hh[:, cols],
+                    scalar=rstd[t][:, 1:2],
+                    in1=beta_cols,
+                    op0=ALU.mult,
+                    op1=ALU.add,
+                )
 
         def add_ih(t, half):
             scaled_ih, scaled_hh = scaled[t]
@@ -341,13 +347,13 @@ def tile_layernormlstmcell_kernel(
         def gate_sigmoids(t):
             gates = scaled[t][0]
             nc.scalar.activation(
-                out=gates[:, 0 : 2 * H], in_=gates[:, 0 : 2 * H], func=ACT.Sigmoid, scale=ROOT_G
+                out=gates[:, 0 : 2 * H], in_=gates[:, 0 : 2 * H], func=ACT.Sigmoid
             )
 
         def gate_tanh(t):
             gates = scaled[t][0]
             nc.scalar.activation(
-                out=gates[:, 2 * H : 3 * H], in_=gates[:, 2 * H : 3 * H], func=ACT.Tanh, scale=ROOT_G
+                out=gates[:, 2 * H : 3 * H], in_=gates[:, 2 * H : 3 * H], func=ACT.Tanh
             )
 
         def gate_functions(t):
@@ -357,7 +363,7 @@ def tile_layernormlstmcell_kernel(
         def output_gate(t):
             o_gate[t] = narrow.tile([P, H], F32, name="o_gate")
             nc.scalar.activation(
-                out=o_gate[t][:], in_=scaled[t][0][:, 3 * H : 4 * H], func=ACT.Sigmoid, scale=ROOT_G
+                out=o_gate[t][:], in_=scaled[t][0][:, 3 * H : 4 * H], func=ACT.Sigmoid
             )
 
         def cell_products(t, engine=nc.gpsimd):
@@ -508,10 +514,10 @@ def tile_layernormlstmcell_kernel(
         with tc.manual_schedule():
             flip_rows(0)
             quantise_rows(0)
-            spread(vector_rows[0], 0, gamma[0], 1.0)
+            spread(vector_rows[0], 0, gamma[0], ROOT_G)
             flip_rows(1)
             quantise_rows(1)
-            spread(vector_rows[1], 0, gamma[1], 1.0)
+            spread(vector_rows[1], 0, gamma[1], ROOT_G)
             for s in range(2):
                 fold_passes(0, s)
                 fold_sum(0, s)
@@ -519,7 +525,9 @@ def tile_layernormlstmcell_kernel(
             flip_rows(2)
             row_means(1)
             quantise_rows(2)
-            spread(vector_rows[2], 1, beta_sum, 1.0 / ROOT_G)
+            for j in range(BETA_BANKS):
+                spread_bank(beta_kept[j][:], vector_rows[2], 1, slice(j * BANK, (j + 1) * BANK))
+            spread(vector_rows[2], 1, beta_sum, 1.0, BETA_BANKS)
             variances(0, -3)
             round_start(1)
             flip_rows(3)

@@ -193,6 +193,7 @@ def tile_layernormlstmcell_kernel(
         o_gate = {}
         c_new = {}
         neg_mean_c = {}
+        sum_c = {}
         rstd_c = {}
         normed = {}
 
@@ -318,11 +319,16 @@ def tile_layernormlstmcell_kernel(
             rstd[gate_tile] = result[:, 0:2]
             rstd_c[cell_tile] = result[:, 2:3]
 
-        def shift_hh(t):
+        def shift_hh(t, first_bank=0, end_bank=BANKS):
             scaled_hh = scaled[t][1]
-            rest = slice(BETA_BANKS * BANK, G)
-            pieces = [(slice(j * BANK, (j + 1) * BANK), beta_kept[j][:]) for j in range(BETA_BANKS)]
-            for cols, beta_cols in pieces + [(rest, beta_sum[:, rest])]:
+            pieces = [
+                (slice(j * BANK, (j + 1) * BANK), beta_kept[j][:])
+                for j in range(first_bank, min(end_bank, BETA_BANKS))
+            ]
+            if end_bank > BETA_BANKS:
+                rest = slice(max(first_bank, BETA_BANKS) * BANK, end_bank * BANK)
+                pieces = pieces + [(rest, beta_sum[:, rest])]
+            for cols, beta_cols in pieces:
                 nc.vector.scalar_tensor_tensor(
                     out=scaled_hh[:, cols],
                     in0=scaled_hh[:, cols],
@@ -333,8 +339,11 @@ def tile_layernormlstmcell_kernel(
                 )
 
         def add_ih(t, half):
+            add_gates(t, 2 * half, 2 * half + 2)
+
+        def add_gates(t, first_bank, end_bank):
             scaled_ih, scaled_hh = scaled[t]
-            cols = slice(half * 2 * H, (half + 1) * 2 * H)
+            cols = slice(first_bank * BANK, end_bank * BANK)
             nc.vector.scalar_tensor_tensor(
                 out=scaled_ih[:, cols],
                 in0=scaled_ih[:, cols],
@@ -367,11 +376,18 @@ def tile_layernormlstmcell_kernel(
             )
 
         def cell_products(t, engine=nc.gpsimd):
+            cell_kept(t, engine)
+            cell_fresh(t, engine)
+
+        def cell_kept(t, engine):
             gates = scaled[t][0]
             kept[t] = narrow.tile([P, H], F32, name="kept")
             engine.tensor_tensor(
                 out=kept[t][:], in0=gates[:, H : 2 * H], in1=c_sb[:, t, :], op=ALU.mult
             )
+
+        def cell_fresh(t, engine):
+            gates = scaled[t][0]
             c_new[t] = narrow.tile([P, H], F32, name="c_new")
             engine.tensor_tensor(
                 out=c_new[t][:], in0=gates[:, 0:H], in1=gates[:, 2 * H : 3 * H], op=ALU.mult
@@ -380,6 +396,23 @@ def tile_layernormlstmcell_kernel(
         def cell_sum(t, engine=nc.gpsimd):
             engine.tensor_tensor(out=c_new[t][:], in0=c_new[t][:], in1=kept[t][:], op=ALU.add)
             nc.sync.dma_start(out=c_out[:, t, :], in_=c_new[t][:])
+
+        def cell_sum_total(t):
+            sum_c[t] = stats.tile([P, 1], F32, name="sum_c")
+            nc.vector.scalar_tensor_tensor(
+                out=c_new[t][:],
+                in0=c_new[t][:],
+                scalar=1.0,
+                in1=kept[t][:],
+                op0=ALU.mult,
+                op1=ALU.add,
+                accum_out=sum_c[t][:],
+            )
+            nc.sync.dma_start(out=c_out[:, t, :], in_=c_new[t][:])
+
+        def cell_mean_of_total(t):
+            neg_mean_c[t] = stats.tile([P, 1], F32, name="neg_mean_c")
+            nc.scalar.activation(out=neg_mean_c[t][:], in_=sum_c[t][:], func=ACT.Copy, scale=-1.0 / H)
 
         def cell_mean(t):
             neg_mean_c[t] = stats.tile([P, 1], F32, name="neg_mean_c")
@@ -549,53 +582,68 @@ def tile_layernormlstmcell_kernel(
                 acc = psum_acc.tile([P, BANK], F32, name="acc")
                 spread_bank(acc[:], vector_rows[2], 2 + v, slice(0, H))
                 nc.scalar.activation(out=cell_spread[:, v, :], in_=acc[:], func=ACT.Copy, scale=factor)
-            for i in range(2, ROW_TILES):
+            last = ROW_TILES - 1
+            for i in range(2, last):
                 round_start(i)
                 round_end(i)
-            last = ROW_TILES - 1
-            cell_turn_back(last - 4)
+            round_start(last)
             cell_products(last - 2)
-            inverse_roots(last, last - 3)
-            cell_sum(last - 2, nc.vector)
-            gate_functions(last - 1)
-            output_gate(last - 1)
+            cell_turn_back(last - 4)
+            shift_hh(last - 1)
+            variances(last, -1)
+            inverse_roots(last, -1)
+            add_ih(last - 1, 0)
+            gate_sigmoids(last - 1)
+            variances(last + SUM_RING, last - 3)
+            inverse_roots(last + SUM_RING, last - 3)
             cell_normalise(last - 3)
             cell_turn(last - 3)
-            shift_hh(last)
-            cell_products(last - 1, nc.vector)
-            add_ih(last, 0)
-            cell_sum(last - 1, nc.vector)
-            add_ih(last, 1)
-            cell_mean(last - 2)
+            shift_hh(last, 0, 2)
+            add_gates(last, 0, 1)
+            shift_hh(last, 2, 3)
+            add_gates(last, 1, 2)
+            gate_sigmoids(last)
+            cell_sum_total(last - 2)
+            add_gates(last, 2, 3)
+            gate_tanh(last)
+            cell_mean_of_total(last - 2)
             cell_squares(last - 2)
-            cell_tanh(last - 3)
-            cell_turn_back(last - 3)
-            hidden_out(last - 4)
-            gate_functions(last)
-            output_gate(last)
-            cell_mean(last - 1)
-            cell_squares(last - 1)
+            add_ih(last - 1, 1)
+            gate_tanh(last - 1)
+            output_gate(last - 1)
             variances(ROW_TILES, last - 2)
             inverse_roots(ROW_TILES, last - 2)
-            cell_products(last, nc.vector)
-            hidden_out(last - 3)
-            cell_sum(last, nc.vector)
+            cell_tanh(last - 3)
+            cell_turn_back(last - 3)
+            cell_kept(last, nc.vector)
+            cell_fresh(last, nc.vector)
+            cell_kept(last - 1, nc.vector)
+            cell_sum_total(last)
+            cell_fresh(last - 1, nc.vector)
+            hidden_out(last - 4)
+            cell_sum_total(last - 1)
+            cell_mean_of_total(last)
+            cell_squares(last)
             cell_normalise(last - 2)
             cell_turn(last - 2)
-            direct_centre(last - 1)
-            variances(ROW_TILES + 1, last - 1)
-            inverse_roots(ROW_TILES + 1, last - 1)
-            cell_mean(last)
-            cell_squares(last)
-            cell_tanh(last - 2)
-            cell_turn_back(last - 2)
+            cell_mean_of_total(last - 1)
+            cell_squares(last - 1)
             direct_centre(last)
-            direct_scale(last - 1)
             variances(ROW_TILES + 2, last)
             inverse_roots(ROW_TILES + 2, last)
-            direct_tanh(last - 1)
+            shift_hh(last, 3, 4)
+            direct_centre(last - 1)
+            add_gates(last, 3, 4)
+            variances(ROW_TILES + 1, last - 1)
+            inverse_roots(ROW_TILES + 1, last - 1)
+            cell_tanh(last - 2)
+            cell_turn_back(last - 2)
             direct_scale(last)
             direct_tanh(last)
-            direct_hidden(last - 1)
+            output_gate(last)
+            hidden_out(last - 3)
+            direct_scale(last - 1)
+            direct_tanh(last - 1)
             hidden_out(last - 2)
             direct_hidden(last)
+            direct_hidden(last - 1)

@@ -197,16 +197,21 @@ def tile_layernormlstmcell_kernel(
         rstd_c = {}
         normed = {}
 
-        def flip_rows(t):
+        def flip_rows(t, on_vector=False):
             flipped = psum_acc.tile([P, 2, 2, P], F32, name="acc")
             for s, rows in enumerate((x_sb, h_sb)):
                 words = rows[:, t, :].bitcast(F32)
                 for u in range(2):
                     nc.tensor.transpose(flipped[:, s, u, :], words[:, u : K // 2 : 2], ident[:])
             grouped[t] = stage.tile([P, 2, P, 4], BF16, name="grouped", align_bytes=64)
-            nc.scalar.copy(
-                out=grouped[t][:].bitcast(F32), in_=flipped[:].rearrange("p s u r -> p s r u")
-            )
+            if on_vector:
+                nc.vector.tensor_copy(
+                    out=grouped[t][:].bitcast(F32), in_=flipped[:].rearrange("p s u r -> p s r u")
+                )
+            else:
+                nc.scalar.copy(
+                    out=grouped[t][:].bitcast(F32), in_=flipped[:].rearrange("p s u r -> p s r u")
+                )
 
         def quantise_rows(t):
             codes = operand.tile([P, 2 * P], U32, align_bytes=64)
@@ -555,14 +560,16 @@ def tile_layernormlstmcell_kernel(
                 fold_passes(0, s)
                 fold_sum(0, s)
                 product(0, s)
-            flip_rows(2)
+            flip_rows(2, True)
             row_means(1)
             quantise_rows(2)
+            variances(0, -3)
+            inverse_roots(0, -3)
+            product(1, 0)
             for j in range(BETA_BANKS):
                 spread_bank(beta_kept[j][:], vector_rows[2], 1, slice(j * BANK, (j + 1) * BANK))
             spread(vector_rows[2], 1, beta_sum, 1.0, BETA_BANKS)
-            variances(0, -3)
-            round_start(1)
+            product(1, 1)
             flip_rows(3)
             round_end(1)
             cols_ps = psum_acc.tile([P, H // P, 2], F32, name="acc")

@@ -118,26 +118,26 @@ def tile_layernormlstmcell_kernel(
             for sbuf, dram in pairs:
                 nc.sync.dma_start(out=sbuf[:, tiles, :], in_=dram[:, tiles, :])
 
-        def load_vector(rows, row, vector):
-            nc.sync.dma_start(
+        def load_vector(rows, row, vector, queue=nc.sync):
+            queue.dma_start(
                 out=rows[row : row + 1, 0 : vector.shape[0]], in_=vector.unsqueeze(0)
             )
 
         def load_weight(s, words, rows):
+            nc.sync.dma_start(
+                out=w_words[s][:].bitcast(I32),
+                in_=words.rearrange("p n t -> p (n t)").bitcast(I32),
+            )
             for quad in range(4):
                 nc.sync.dma_start(
                     out=w_scales[s][32 * quad : 32 * quad + 4, :].bitcast(I32),
                     in_=rows[4 * quad : 4 * quad + 4, :].bitcast(I32),
                 )
-            nc.sync.dma_start(
-                out=w_words[s][:].bitcast(I32),
-                in_=words.rearrange("p n t -> p (n t)").bitcast(I32),
-            )
 
         load_rows(slice(0, FIRST_TILES), (x_sb, x_rows), (h_sb, h_rows))
-        load_vector(vector_rows[0], 0, gamma_ih)
+        load_vector(vector_rows[0], 0, gamma_ih, nc.scalar)
         load_weight(0, W_ih_words[0], W_ih_scales[0])
-        load_vector(vector_rows[1], 0, gamma_hh)
+        load_vector(vector_rows[1], 0, gamma_hh, nc.scalar)
         load_weight(1, W_hh_words[0], W_hh_scales[0])
         load_vector(vector_rows[2], 0, beta_ih)
         load_vector(vector_rows[2], 1, beta_hh)

from contextlib import ExitStack

import concourse.mybir as mybir
from concourse.masks import make_identity

F32 = mybir.dt.float32
BF16 = mybir.dt.bfloat16
I32 = mybir.dt.int32
U32 = mybir.dt.uint32
U8 = mybir.dt.uint8
FP8X4 = mybir.dt.float8_e4m3fn_x4
ALU = mybir.AluOpType
ACT = mybir.ActivationFunctionType
AX = mybir.AxisListType

P = 128
B = 2048
K = 512
H = 512
G = 4 * H
EPS = 1e-5
ROW_TILES = B // P
BANK = 512
BANKS = G // BANK
FOLD = 128
LOAD_TILES = 4
FIRST_TILES = 2
ROOT_G = G**0.5
BETA_BANKS = 2
ROOT_H = H**0.5
SUM_RING = 4

FLOPS = 2 * 2 * B * K * G


def tile_layernormlstmcell_kernel(
    tc,
    x,
    h_prev,
    c_prev,
    W_ih_words,
    W_ih_scales,
    W_hh_words,
    W_hh_scales,
    gamma_ih,
    beta_ih,
    gamma_hh,
    beta_hh,
    gamma_c,
    beta_c,
    out_0,
    out_1,
):
    nc = tc.nc
    with ExitStack() as ctx:
        const = ctx.enter_context(tc.tile_pool(name="const", bufs=1))
        stage = ctx.enter_context(tc.tile_pool(name="stage", bufs=2))
        operand = ctx.enter_context(tc.tile_pool(name="operand", bufs=4))
        stats = ctx.enter_context(tc.tile_pool(name="stats", bufs=4))
        wide_ih = ctx.enter_context(tc.tile_pool(name="wide_ih", bufs=4))
        wide_hh = ctx.enter_context(tc.tile_pool(name="wide_hh", bufs=2))
        narrow = ctx.enter_context(tc.tile_pool(name="narrow", bufs=4))
        psum_acc = ctx.enter_context(tc.psum_pool(name="psum_acc", bufs=8 - BETA_BANKS))
        psum_keep = ctx.enter_context(tc.psum_pool(name="psum_keep", bufs=1))

        x_rows = x.rearrange("(p t) k -> p t k", t=ROW_TILES)
        h_rows = h_prev.rearrange("(p t) k -> p t k", t=ROW_TILES)
        c_rows = c_prev.rearrange("(p t) k -> p t k", t=ROW_TILES)
        h_out = out_0.rearrange("(p t) k -> p t k", t=ROW_TILES)
        c_out = out_1.rearrange("(p t) k -> p t k", t=ROW_TILES)

        zero = const.tile([P, 1], F32)
        nc.vector.memset(zero[:], 0.0)
        warm = const.tile([P, 1], F32)
        nc.scalar.activation(out=warm[:], in_=zero[:], func=ACT.Sigmoid)

        vector_rows = [
            const.tile([P, G], BF16, name="gamma_ih_row"),
            const.tile([P, G], BF16, name="gamma_hh_row"),
            const.tile([P, G], BF16, name="late_rows"),
        ]
        w_scales = [
            const.tile([P, G], U8, name="w_ih_scales", align_bytes=64),
            const.tile([P, G], U8, name="w_hh_scales", align_bytes=64),
        ]
        for zeroed in (vector_rows[0], w_scales[0], vector_rows[1], w_scales[1], vector_rows[2]):
            nc.vector.memset(zeroed[:].bitcast(I32), 0)
        minus_half = const.tile([P, 3], F32)
        nc.vector.memset(minus_half[:], -0.5)
        sums = [const.tile([P, 3, BANKS + 1], F32, name="sums%d" % r) for r in range(SUM_RING)]
        for ring_tile in sums:
            nc.vector.memset(ring_tile[:], 0.0)
        for ring_tile in sums:
            for rows, length in ((slice(0, 2), G), (slice(2, 3), H)):
                nc.vector.tensor_scalar(
                    out=ring_tile[:, rows, BANKS : BANKS + 1],
                    in0=ring_tile[:, rows, BANKS : BANKS + 1],
                    scalar1=1.0,
                    scalar2=EPS * length,
                    op0=ALU.mult,
                    op1=ALU.add,
                )
        ident = const.tile([P, P], F32)
        make_identity(nc, ident[:])
        pick = const.tile([P, 4], BF16)
        nc.scalar.copy(out=pick[:], in_=ident[:, 0:4])
        nc.vector.tensor_tensor(out=pick[:, 1:2], in0=ident[:, 0:1], in1=ident[:, 1:2], op=ALU.add)

        x_sb = const.tile([P, ROW_TILES, K], BF16)
        h_sb = const.tile([P, ROW_TILES, K], BF16)
        c_sb = const.tile([P, ROW_TILES, H], BF16)
        w_words = [
            const.tile([P, 4 * G], U8, name="w_ih_words", align_bytes=64),
            const.tile([P, 4 * G], U8, name="w_hh_words", align_bytes=64),
        ]

        def load_rows(tiles, *pairs):
            for sbuf, dram in pairs:
                nc.sync.dma_start(out=sbuf[:, tiles, :], in_=dram[:, tiles, :])

        def load_vector(rows, row, vector, queue=nc.sync):
            queue.dma_start(
                out=rows[row : row + 1, 0 : vector.shape[0]], in_=vector.unsqueeze(0)
            )

        def load_weight(s, words, rows):
            nc.sync.dma_start(
                out=w_words[s][:].bitcast(I32),
                in_=words.rearrange("p n t -> p (n t)").bitcast(I32),
            )
            for quad in range(4):
                nc.sync.dma_start(
                    out=w_scales[s][32 * quad : 32 * quad + 4, :].bitcast(I32),
                    in_=rows[4 * quad : 4 * quad + 4, :].bitcast(I32),
                )

        load_rows(slice(0, FIRST_TILES), (x_sb, x_rows), (h_sb, h_rows))
        load_vector(vector_rows[0], 0, gamma_ih, nc.scalar)
        load_weight(0, W_ih_words[0], W_ih_scales[0])
        load_vector(vector_rows[1], 0, gamma_hh, nc.scalar)
        load_weight(1, W_hh_words[0], W_hh_scales[0])
        load_vector(vector_rows[2], 0, beta_ih)
        load_vector(vector_rows[2], 1, beta_hh)
        load_rows(slice(FIRST_TILES, LOAD_TILES), (x_sb, x_rows), (h_sb, h_rows))
        load_vector(vector_rows[2], 2, gamma_c)
        load_vector(vector_rows[2], 3, beta_c)
        load_rows(slice(0, LOAD_TILES), (c_sb, c_rows))
        for start in range(LOAD_TILES, ROW_TILES, LOAD_TILES):
            load_rows(slice(start, start + LOAD_TILES), (x_sb, x_rows), (h_sb, h_rows), (c_sb, c_rows))

        gamma = [
            const.tile([P, G], F32, name="gamma_ih_sb"),
            const.tile([P, G], F32, name="gamma_hh_sb"),
        ]
        beta_sum = const.tile([P, G], F32)
        beta_kept = [psum_keep.tile([P, BANK], F32, name="beta_kept%d" % j) for j in range(BETA_BANKS)]
        cell_cols = const.tile([P, H // P, 2], F32)
        cell_spread = const.tile([P, 2, H], F32)

        def spread_bank(acc, rows, r, cols):
            nc.tensor.matmul(
                out=acc,
                lhsT=pick[:, r : r + 1].to_broadcast([P, P]),
                rhs=rows[:, cols],
                start=True,
                stop=True,
            )

        def spread(rows, r, out, factor, first_bank=0):
            for j in range(first_bank, BANKS):
                cols = slice(j * BANK, (j + 1) * BANK)
                acc = psum_acc.tile([P, BANK], F32, name="acc")
                spread_bank(acc[:], rows, r, cols)
                if j % 2 == 0:
                    nc.scalar.activation(out=out[:, cols], in_=acc[:], func=ACT.Copy, scale=factor)
                else:
                    nc.vector.tensor_scalar(
                        out=out[:, cols], in0=acc[:], scalar1=factor, scalar2=None, op0=ALU.mult
                    )

        grouped = {}
        shift_c = {}
        turned = {}
        tanh_t = {}
        back = {}
        fold = {}
        rows_mx = {}
        neg_mean = {}
        var = {}
        kept = {}
        scaled = {}
        rstd = {}
        o_gate = {}
        c_new = {}
        neg_mean_c = {}
        sum_c = {}
        rstd_c = {}
        normed = {}

        def flip_rows(t, on_vector=False):
            flipped = psum_acc.tile([P, 2, 2, P], F32, name="acc")
            for s, rows in enumerate((x_sb, h_sb)):
                words = rows[:, t, :].bitcast(F32)
                for u in range(2):
                    nc.tensor.transpose(flipped[:, s, u, :], words[:, u : K // 2 : 2], ident[:])
            grouped[t] = stage.tile([P, 2, P, 4], BF16, name="grouped", align_bytes=64)
            if on_vector:
                nc.vector.tensor_copy(
                    out=grouped[t][:].bitcast(F32), in_=flipped[:].rearrange("p s u r -> p s r u")
                )
            else:
                nc.scalar.copy(
                    out=grouped[t][:].bitcast(F32), in_=flipped[:].rearrange("p s u r -> p s r u")
                )

        def quantise_rows(t):
            codes = operand.tile([P, 2 * P], U32, align_bytes=64)
            scales = operand.tile([P, 2 * P], U8, align_bytes=64)
            nc.vector.quantize_mx(
                out=codes[:].bitcast(FP8X4),
                scales=scales[:],
                in_=grouped[t][:].rearrange("p s r t -> p (s r t)"),
            )
            rows_mx[t] = (codes, scales)

        def mx_pass(out, t, s, col, width, start, stop):
            codes, scales = rows_mx[t]
            rows = slice(s * P, (s + 1) * P)
            nc.tensor.matmul_mx(
                out=out,
                lhsT=codes[:, rows].bitcast(FP8X4),
                lhsT_scale=scales[:, rows],
                rhs=w_words[s][:, 4 * col : 4 * (col + width)].bitcast(FP8X4),
                rhs_scale=w_scales[s][:, col : col + width],
                start=start,
                stop=stop,
            )

        def fold_passes(t, s):
            if s == 0:
                fold[t] = psum_acc.tile([P, 2, FOLD], F32, name="acc")
            for j in range(G // FOLD):
                mx_pass(fold[t][:, s, :], t, s, j * FOLD, FOLD, j == 0, j == G // FOLD - 1)

        def fold_sum(t, s):
            if s == 0:
                neg_mean[t] = stats.tile([P, 2], F32, name="neg_mean")
            scrap = stage.tile([P, BANK], BF16, name="scrap")
            nc.scalar.activation(
                out=scrap[:, 0:FOLD],
                in_=fold[t][:, s, :],
                func=ACT.Copy,
                scale=-1.0 / G,
                accum_out=neg_mean[t][:, s : s + 1],
            )

        def row_means(t):
            for s in range(2):
                fold_passes(t, s)
            for s in range(2):
                fold_sum(t, s)

        def product(t, s):
            if s == 0:
                scaled[t] = (
                    wide_ih.tile([P, G], F32, name="scaled_ih"),
                    wide_hh.tile([P, G], F32, name="scaled_hh"),
                )
            for j in range(BANKS):
                cols = slice(j * BANK, (j + 1) * BANK)
                acc = psum_acc.tile([P, BANK], F32, name="acc")
                mx_pass(acc[:], t, s, j * BANK, BANK, True, True)
                nc.vector.scalar_tensor_tensor(
                    out=scaled[t][s][:, cols],
                    in0=acc[:],
                    scalar=neg_mean[t][:, s : s + 1],
                    in1=gamma[s][:, cols],
                    op0=ALU.add,
                    op1=ALU.mult,
                )
                scrap = stage.tile([P, BANK], BF16, name="scrap")
                nc.scalar.activation(
                    out=scrap[:],
                    in_=acc[:],
                    func=ACT.Square,
                    bias=neg_mean[t][:, s : s + 1],
                    accum_out=sums[t % SUM_RING][:, s, j : j + 1],
                )

        def products(t):
            product(t, 0)
            product(t, 1)

        def live_columns(gate_tile, cell_tile):
            first_col = 0 if 0 <= gate_tile < ROW_TILES else 2
            end_col = 3 if 0 <= cell_tile < ROW_TILES else 2
            return first_col, end_col

        def variances(gate_tile, cell_tile):
            first_col, end_col = live_columns(gate_tile, cell_tile)
            if first_col == end_col:
                return
            live = slice(first_col, end_col)
            var[gate_tile] = stats.tile([P, 3], F32, name="var")
            nc.vector.tensor_reduce(
                out=var[gate_tile][:, live],
                in_=sums[gate_tile % SUM_RING][:, live, :],
                axis=AX.X,
                op=ALU.add,
            )

        def inverse_roots(gate_tile, cell_tile):
            first_col, end_col = live_columns(gate_tile, cell_tile)
            if first_col == end_col:
                return
            live = slice(first_col, end_col)
            result = stats.tile([P, 3], F32)
            nc.gpsimd.tensor_tensor(
                out=result[:, live],
                in0=var[gate_tile][:, live],
                in1=minus_half[:, live],
                op=ALU.pow,
            )
            rstd[gate_tile] = result[:, 0:2]
            rstd_c[cell_tile] = result[:, 2:3]

        def shift_hh(t, first_bank=0, end_bank=BANKS):
            scaled_hh = scaled[t][1]
            pieces = [
                (slice(j * BANK, (j + 1) * BANK), beta_kept[j][:])
                for j in range(first_bank, min(end_bank, BETA_BANKS))
            ]
            if end_bank > BETA_BANKS:
                rest = slice(max(first_bank, BETA_BANKS) * BANK, end_bank * BANK)
                pieces = pieces + [(rest, beta_sum[:, rest])]
            for cols, beta_cols in pieces:
                nc.vector.scalar_tensor_tensor(
                    out=scaled_hh[:, cols],
                    in0=scaled_hh[:, cols],
                    scalar=rstd[t][:, 1:2],
                    in1=beta_cols,
                    op0=ALU.mult,
                    op1=ALU.add,
                )

        def add_ih(t, half):
            add_gates(t, 2 * half, 2 * half + 2)

        def add_gates(t, first_bank, end_bank):
            scaled_ih, scaled_hh = scaled[t]
            cols = slice(first_bank * BANK, end_bank * BANK)
            nc.vector.scalar_tensor_tensor(
                out=scaled_ih[:, cols],
                in0=scaled_ih[:, cols],
                scalar=rstd[t][:, 0:1],
                in1=scaled_hh[:, cols],
                op0=ALU.mult,
                op1=ALU.add,
            )

        def gate_sigmoids(t):
            gates = scaled[t][0]
            nc.scalar.activation(
                out=gates[:, 0 : 2 * H], in_=gates[:, 0 : 2 * H], func=ACT.Sigmoid
            )

        def gate_tanh(t):
            gates = scaled[t][0]
            nc.scalar.activation(
                out=gates[:, 2 * H : 3 * H], in_=gates[:, 2 * H : 3 * H], func=ACT.Tanh
            )

        def gate_functions(t):
            gate_sigmoids(t)
            gate_tanh(t)

        def output_gate(t):
            o_gate[t] = narrow.tile([P, H], F32, name="o_gate")
            nc.scalar.activation(
                out=o_gate[t][:], in_=scaled[t][0][:, 3 * H : 4 * H], func=ACT.Sigmoid
            )

        def cell_products(t, engine=nc.gpsimd):
            cell_kept(t, engine)
            cell_fresh(t, engine)

        def cell_kept(t, engine):
            gates = scaled[t][0]
            kept[t] = narrow.tile([P, H], F32, name="kept")
            engine.tensor_tensor(
                out=kept[t][:], in0=gates[:, H : 2 * H], in1=c_sb[:, t, :], op=ALU.mult
            )

        def cell_fresh(t, engine):
            gates = scaled[t][0]
            c_new[t] = narrow.tile([P, H], F32, name="c_new")
            engine.tensor_tensor(
                out=c_new[t][:], in0=gates[:, 0:H], in1=gates[:, 2 * H : 3 * H], op=ALU.mult
            )

        def cell_sum(t, engine=nc.gpsimd):
            engine.tensor_tensor(out=c_new[t][:], in0=c_new[t][:], in1=kept[t][:], op=ALU.add)
            nc.sync.dma_start(out=c_out[:, t, :], in_=c_new[t][:])

        def cell_sum_total(t):
            sum_c[t] = stats.tile([P, 1], F32, name="sum_c")
            nc.vector.scalar_tensor_tensor(
                out=c_new[t][:],
                in0=c_new[t][:],
                scalar=1.0,
                in1=kept[t][:],
                op0=ALU.mult,
                op1=ALU.add,
                accum_out=sum_c[t][:],
            )
            nc.sync.dma_start(out=c_out[:, t, :], in_=c_new[t][:])

        def cell_mean_of_total(t):
            neg_mean_c[t] = stats.tile([P, 1], F32, name="neg_mean_c")
            nc.scalar.activation(out=neg_mean_c[t][:], in_=sum_c[t][:], func=ACT.Copy, scale=-1.0 / H)

        def cell_mean(t):
            neg_mean_c[t] = stats.tile([P, 1], F32, name="neg_mean_c")
            scrap = stage.tile([P, BANK], BF16, name="scrap")
            nc.scalar.activation(
                out=scrap[:],
                in_=c_new[t][:],
                func=ACT.Copy,
                scale=-1.0 / H,
                accum_out=neg_mean_c[t][:],
            )

        def cell_squares(t):
            scrap = stage.tile([P, BANK], BF16, name="scrap")
            nc.scalar.activation(
                out=scrap[:],
                in_=c_new[t][:],
                func=ACT.Square,
                bias=neg_mean_c[t][:],
                accum_out=sums[(t + 3) % SUM_RING][:, 2, 0:1],
            )

        def cell_shift(t):
            shift_c[t] = stats.tile([P, 1], F32, name="shift_c")
            nc.scalar.activation(out=shift_c[t][:], in_=neg_mean_c[t][:], func=ACT.Copy, scale=rstd_c[t])

        def cell_scale(t):
            normed[t] = narrow.tile([P, H], F32, name="normed")
            nc.scalar.activation(
                out=normed[t][:], in_=c_new[t][:], func=ACT.Identity, scale=rstd_c[t], bias=shift_c[t][:]
            )

        def cell_normalise(t):
            cell_shift(t)
            cell_scale(t)

        def cell_normalise_beside(t):
            normed[t] = narrow.tile([P, H], F32, name="normed")
            nc.gpsimd.tensor_scalar(
                out=normed[t][:],
                in0=c_new[t][:],
                scalar1=neg_mean_c[t][:],
                scalar2=rstd_c[t],
                op0=ALU.add,
                op1=ALU.mult,
            )

        def cell_turn(t):
            turned[t] = psum_acc.tile([P, H // P, P], F32, name="acc")
            for b in range(H // P):
                nc.tensor.transpose(turned[t][:, b, :], normed[t][:, b * P : (b + 1) * P], ident[:])

        def cell_tanh(t):
            tanh_t[t] = narrow.tile([P, H // P, P], F32, name="tanh_t")
            for b in range(H // P):
                nc.scalar.activation(
                    out=tanh_t[t][:, b, :],
                    in_=turned[t][:, b, :],
                    func=ACT.Tanh,
                    scale=cell_cols[:, b, 0:1],
                    bias=cell_cols[:, b, 1:2],
                )

        def cell_turn_back(t):
            back[t] = psum_acc.tile([P, H], F32, name="acc")
            for b in range(H // P):
                nc.tensor.transpose(back[t][:, b * P : (b + 1) * P], tanh_t[t][:, b, :], ident[:])

        def hidden_out(t):
            h_new = narrow.tile([P, H], F32)
            nc.vector.tensor_tensor(out=h_new[:], in0=o_gate[t][:], in1=back[t][:], op=ALU.mult)
            nc.sync.dma_start(out=h_out[:, t, :], in_=h_new[:])

        def direct_centre(t):
            normed[t] = narrow.tile([P, H], F32, name="normed")
            nc.vector.scalar_tensor_tensor(
                out=normed[t][:],
                in0=c_new[t][:],
                scalar=neg_mean_c[t][:],
                in1=cell_spread[:, 0, :],
                op0=ALU.add,
                op1=ALU.mult,
            )

        def direct_scale(t):
            nc.vector.scalar_tensor_tensor(
                out=normed[t][:],
                in0=normed[t][:],
                scalar=rstd_c[t],
                in1=cell_spread[:, 1, :],
                op0=ALU.mult,
                op1=ALU.add,
            )

        def direct_tanh(t):
            nc.scalar.activation(out=normed[t][:], in_=normed[t][:], func=ACT.Tanh, scale=ROOT_H)

        def direct_hidden(t):
            h_new = narrow.tile([P, H], F32, name="h_new")
            nc.vector.tensor_tensor(out=h_new[:], in0=o_gate[t][:], in1=normed[t][:], op=ALU.mult)
            nc.sync.dma_start(out=h_out[:, t, :], in_=h_new[:])

        def on(stage_of, t, *more):
            if 0 <= t < ROW_TILES:
                stage_of(t, *more)

        def round_start(i):
            on(gate_sigmoids, i - 2)
            on(cell_products, i - 3)
            inverse_roots(i - 1, i - 4)
            on(cell_sum, i - 3)
            on(cell_normalise_beside, i - 4)
            on(gate_tanh, i - 2)
            on(products, i)
            on(cell_turn_back, i - 5)
            on(cell_turn, i - 4)
            on(hidden_out, i - 5)
            on(cell_mean, i - 3)
            on(output_gate, i - 2)
            on(cell_squares, i - 3)
            on(cell_tanh, i - 4)

        def round_end(i):
            on(shift_hh, i - 1)
            on(quantise_rows, i + 2)
            on(add_ih, i - 1, 0)
            on(add_ih, i - 1, 1)
            variances(i, i - 3)
            on(row_means, i + 1)
            on(flip_rows, i + 3)

        with tc.manual_schedule():
            flip_rows(0)
            quantise_rows(0)
            spread(vector_rows[0], 0, gamma[0], ROOT_G)
            flip_rows(1)
            quantise_rows(1)
            spread(vector_rows[1], 0, gamma[1], ROOT_G)
            for s in range(2):
                fold_passes(0, s)
                fold_sum(0, s)
                product(0, s)
            flip_rows(2, True)
            row_means(1)
            quantise_rows(2)
            variances(0, -3)
            inverse_roots(0, -3)
            product(1, 0)
            for j in range(BETA_BANKS):
                spread_bank(beta_kept[j][:], vector_rows[2], 1, slice(j * BANK, (j + 1) * BANK))
            spread(vector_rows[2], 1, beta_sum, 1.0, BETA_BANKS)
            product(1, 1)
            flip_rows(3)
            round_end(1)
            cols_ps = psum_acc.tile([P, H // P, 2], F32, name="acc")
            for b in range(H // P):
                nc.tensor.matmul(
                    out=cols_ps[:, b, :],
                    lhsT=vector_rows[2][:, b * P : (b + 1) * P],
                    rhs=pick[:, 2:4],
                    start=True,
                    stop=True,
                )
            nc.scalar.activation(
                out=cell_cols[:, :, 0:1], in_=cols_ps[:, :, 0:1], func=ACT.Copy, scale=ROOT_H
            )
            nc.scalar.copy(out=cell_cols[:, :, 1:2], in_=cols_ps[:, :, 1:2])
            for v, factor in enumerate((1.0, 1.0 / ROOT_H)):
                acc = psum_acc.tile([P, BANK], F32, name="acc")
                spread_bank(acc[:], vector_rows[2], 2 + v, slice(0, H))
                nc.scalar.activation(out=cell_spread[:, v, :], in_=acc[:], func=ACT.Copy, scale=factor)
            last = ROW_TILES - 1
            for i in range(2, last):
                round_start(i)
                round_end(i)
            round_start(last)
            cell_products(last - 2)
            cell_turn_back(last - 4)
            shift_hh(last - 1)
            variances(last, -1)
            inverse_roots(last, -1)
            add_ih(last - 1, 0)
            gate_sigmoids(last - 1)
            variances(last + SUM_RING, last - 3)
            inverse_roots(last + SUM_RING, last - 3)
            cell_normalise(last - 3)
            cell_turn(last - 3)
            shift_hh(last, 0, 2)
            add_gates(last, 0, 1)
            shift_hh(last, 2, 3)
            add_gates(last, 1, 2)
            gate_sigmoids(last)
            cell_sum_total(last - 2)
            add_gates(last, 2, 3)
            gate_tanh(last)
            cell_mean_of_total(last - 2)
            cell_squares(last - 2)
            add_ih(last - 1, 1)
            gate_tanh(last - 1)
            output_gate(last - 1)
            variances(ROW_TILES, last - 2)
            inverse_roots(ROW_TILES, last - 2)
            cell_tanh(last - 3)
            cell_turn_back(last - 3)
            cell_kept(last, nc.vector)
            cell_fresh(last, nc.vector)
            cell_kept(last - 1, nc.vector)
            cell_sum_total(last)
            cell_fresh(last - 1, nc.vector)
            hidden_out(last - 4)
            cell_sum_total(last - 1)
            cell_mean_of_total(last)
            cell_squares(last)
            cell_normalise(last - 2)
            cell_turn(last - 2)
            cell_mean_of_total(last - 1)
            cell_squares(last - 1)
            direct_centre(last)
            variances(ROW_TILES + 2, last)
            inverse_roots(ROW_TILES + 2, last)
            shift_hh(last, 3, 4)
            direct_centre(last - 1)
            add_gates(last, 3, 4)
            variances(ROW_TILES + 1, last - 1)
            inverse_roots(ROW_TILES + 1, last - 1)
            cell_tanh(last - 2)
            cell_turn_back(last - 2)
            direct_scale(last)
            direct_tanh(last)
            output_gate(last)
            hidden_out(last - 3)
            direct_scale(last - 1)
            direct_tanh(last - 1)
            hidden_out(last - 2)
            direct_hidden(last)
            direct_hidden(last - 1)
